import numpy as np
import ml_dtypes


def mxq(x, axis, fmt="e4m3"):
    dtype, down = {"e4m3": (ml_dtypes.float8_e4m3fn, 7), "e5m2": (ml_dtypes.float8_e5m2, 14)}[fmt]
    v = np.moveaxis(np.asarray(x, np.float32).astype(ml_dtypes.bfloat16).astype(np.float64), axis, -1)
    blocks = v.reshape(v.shape[:-1] + (-1, 32))
    amax = np.abs(blocks).max(-1, keepdims=True)
    byte = np.maximum(np.where(amax > 0, np.frexp(amax)[1] - 1 + 127, 0) - down, 1)
    scale = np.exp2(byte - 127.0)
    codes = (blocks / scale).astype(np.float32).astype(dtype).astype(np.float64)
    return np.moveaxis((codes * scale).reshape(v.shape), -1, axis)


WIDE = False


def mx_kscale(k):
    if not WIDE:
        return np.ones(k)
    levels = np.array([10, -10, 5, -5, 0])
    if k % 512:
        return np.exp2(np.random.permutation(np.resize(levels, k // 32))).repeat(32)
    a = np.empty((k // 512, 16))
    for p in range(k // 512):
        a[p, :8] = np.random.permutation(np.resize(levels, 8))
        for g in range(8):
            far = levels[np.abs(levels - a[p, g]) >= 10]
            a[p, g + 8] = far[np.random.randint(len(far))]
    return np.exp2(a.ravel()).repeat(32)


BF16 = ml_dtypes.bfloat16


def bf(x):
    return np.asarray(x, np.float32).astype(BF16)


def f64(x):
    return np.asarray(x).astype(np.float64)


B, T, C, NH, HS, NLQ, NLKV, DHR = 4, 1024, 512, 4, 128, 512, 512, 128


def setup_inputs():
    s, t = mx_kscale(C), mx_kscale(NLKV)
    return {"y_lat": bf(np.random.standard_normal((B, NH, T, NLKV)) * 0.35 / t),
            "W_uv": bf(np.random.standard_normal((C, NLKV)) * 2.0 / np.sqrt(NLKV) * s[:, None] * t[None, :]),
            "W_o": bf(np.random.standard_normal((C, C)) / np.sqrt(C) / s[None, :])}


def reference(y_lat, W_uv, W_o):
    v_flat = mxq(f64(W_uv), 0, "e4m3").T @ mxq(f64(W_o), 1, "e4m3").T
    v_eff = v_flat.reshape(NLKV, NH, HS).transpose(1, 0, 2)
    y = mxq(f64(y_lat), 3, "e4m3") @ mxq(v_eff, 1, "e4m3")[None]
    return y.transpose(0, 2, 1, 3).reshape(B, T, C)

@@ -1,0 +1,185 @@
+from contextlib import ExitStack
+
+import concourse.mybir as mybir
+from concourse.masks import make_identity
+
+BF16 = mybir.dt.bfloat16
+F32 = mybir.dt.float32
+U32 = mybir.dt.uint32
+U8 = mybir.dt.uint8
+FP8X4 = mybir.dt.float8_e4m3fn_x4
+
+P = 128
+PACK = 4
+K = P * PACK
+WORDS = K // 2
+HALVES = WORDS // P
+
+B, NH, T, HS = 4, 4, 1024, 128
+C = NH * HS
+Y_TILES = B * NH
+ROW_TILES = T // P
+PAIR = 2
+GROUPS_PER_BANK = 4
+
+Y_TILES_IN_SBUF = 12
+MULTIPLY_LAG = 2
+
+FLOPS = 2 * K * K * C + 2 * B * NH * T * K * HS
+
+
+def transpose_rows(nc, pools, identity, rows, row_tiles):
+    row_words = rows.bitcast(F32)
+    grouped = pools["grouped"].tile([P, row_tiles * P * PACK], BF16, tag="grouped", align_bytes=64)
+    grouped_words = grouped[:].bitcast(F32)
+    bank_words = PAIR * P * HALVES
+    for pair in range(row_tiles // PAIR):
+        planes = pools["planes"].tile([P, HALVES, PAIR * P], F32, tag="planes")
+        for i in range(PAIR):
+            for u in range(HALVES):
+                word = (pair * PAIR + i) * WORDS
+                nc.tensor.transpose(
+                    planes[:, u, i * P : (i + 1) * P],
+                    row_words[:, word + u : word + WORDS : HALVES],
+                    identity,
+                )
+        nc.scalar.copy(
+            out=grouped_words[:, pair * bank_words : (pair + 1) * bank_words].rearrange(
+                "p (n u) -> p n u", u=HALVES
+            ),
+            in_=planes[:].rearrange("p u n -> p n u"),
+        )
+    return grouped
+
+
+def quantise(nc, grouped, codes, scales):
+    nc.vector.quantize_mx(out=codes[:].bitcast(FP8X4), scales=scales[:], in_=grouped[:])
+
+
+def tile_causalselfattention_pc_t_kernel(tc, y_lat, W_uv, W_o, out):
+    nc = tc.nc
+    with ExitStack() as ctx:
+        keep = ctx.enter_context(tc.tile_pool(name="keep", bufs=1))
+        y_pool = ctx.enter_context(tc.tile_pool(name="y_rows", bufs=Y_TILES_IN_SBUF))
+        out_pool = ctx.enter_context(tc.tile_pool(name="result", bufs=B))
+        mx_pool = ctx.enter_context(tc.tile_pool(name="mx", bufs=3))
+        pools = {
+            "grouped": ctx.enter_context(tc.tile_pool(name="grouped", bufs=3)),
+            "planes": ctx.enter_context(tc.psum_pool(name="planes", bufs=4)),
+        }
+        acc_pool = ctx.enter_context(tc.psum_pool(name="acc", bufs=4))
+
+        identity = keep.tile([P, P], F32)
+        make_identity(nc, identity[:])
+
+        uv_rows = keep.tile([P, PACK, K], BF16)
+        nc.sync.dma_start(out=uv_rows[:], in_=W_uv.rearrange("(p t) l -> p t l", t=PACK))
+        wo_rows = keep.tile([P, NH * K], BF16)
+        nc.sync.dma_start(
+            out=wo_rows[:].rearrange("p (h j) -> p h j", h=NH),
+            in_=W_o.rearrange("(h p) j -> p h j", p=P),
+        )
+
+        y_rows = {}
+
+        def load_y(n):
+            y_rows[n] = y_pool.tile([P, ROW_TILES * K], BF16, name="y_rows")
+            nc.sync.dma_start(
+                out=y_rows[n][:],
+                in_=y_lat[n // NH, n % NH].rearrange("(p i) l -> p (i l)", i=ROW_TILES),
+            )
+
+        for n in range(Y_TILES_IN_SBUF):
+            load_y(n)
+
+        wo_grouped = transpose_rows(nc, pools, identity[:], wo_rows[:], NH)
+
+        uv_grouped = pools["grouped"].tile([P, K * PACK], BF16, tag="grouped", align_bytes=64)
+        uv_by_code = uv_rows[:].rearrange("p t (m c) -> p c m t", c=PACK)
+        for code in range(PACK):
+            nc.vector.tensor_copy(
+                out=uv_grouped[:, code * K : (code + 1) * K].rearrange("p (m t) -> p m t", t=PACK),
+                in_=uv_by_code[:, code],
+            )
+        uv_codes = keep.tile([P, K], U32, align_bytes=64)
+        uv_scales = keep.tile([P, K], U8, align_bytes=64)
+        quantise(nc, uv_grouped, uv_codes, uv_scales)
+        wo_codes = keep.tile([P, C], U32, align_bytes=64)
+        wo_scales = keep.tile([P, C], U8, align_bytes=64)
+        quantise(nc, wo_grouped, wo_codes, wo_scales)
+
+        y_grouped, y_codes, y_scales, y_acc, results = {}, {}, {}, {}, {}
+        v_codes = keep.tile([P, C], U32, align_bytes=64)
+        v_scales = keep.tile([P, C], U8, align_bytes=64)
+
+        def transpose_y(n):
+            y_grouped[n] = transpose_rows(nc, pools, identity[:], y_rows[n][:], ROW_TILES)
+
+        def quantise_y(n):
+            y_codes[n] = mx_pool.tile([P, ROW_TILES * P], U32, name="y_codes", align_bytes=64)
+            y_scales[n] = mx_pool.tile([P, ROW_TILES * P], U8, name="y_scales", align_bytes=64)
+            quantise(nc, y_grouped[n], y_codes[n], y_scales[n])
+
+        def multiply_y(n):
+            head = slice((n % NH) * HS, (n % NH + 1) * HS)
+            y_acc[n] = []
+            for first in range(0, ROW_TILES, GROUPS_PER_BANK):
+                acc = acc_pool.tile([P, GROUPS_PER_BANK, HS], F32, tag="acc")
+                for g in range(GROUPS_PER_BANK):
+                    tokens = slice((first + g) * P, (first + g + 1) * P)
+                    nc.tensor.matmul_mx(
+                        out=acc[:, g, :],
+                        lhsT=y_codes[n][:, tokens].bitcast(FP8X4),
+                        lhsT_scale=y_scales[n][:, tokens],
+                        rhs=v_codes[:, head].bitcast(FP8X4),
+                        rhs_scale=v_scales[:, head],
+                        start=True,
+                        stop=True,
+                    )
+                y_acc[n].append(acc)
+
+        def empty_y(n):
+            b, h = n // NH, n % NH
+            if h == 0:
+                results[b] = out_pool.tile([P, ROW_TILES, C], F32, name="result")
+            out_rows = out[b].rearrange("(p i) c -> p i c", i=ROW_TILES)
+            for bank, acc in enumerate(y_acc[n]):
+                done = slice(bank * GROUPS_PER_BANK, (bank + 1) * GROUPS_PER_BANK)
+                nc.vector.tensor_copy(out=results[b][:, done, h * HS : (h + 1) * HS], in_=acc[:])
+                if h == NH - 1:
+                    nc.sync.dma_start(out=out_rows[:, done, :], in_=results[b][:, done, :])
+
+        transpose_y(0)
+
+        v_grouped = pools["grouped"].tile([P, C * PACK], BF16, tag="grouped", align_bytes=64)
+        for h in range(NH):
+            head = slice(h * HS, (h + 1) * HS)
+            v_acc = acc_pool.tile([P, PACK, HS], F32, tag="acc")
+            for code in range(PACK):
+                latent = slice(code * P, (code + 1) * P)
+                nc.tensor.matmul_mx(
+                    out=v_acc[:, code, :],
+                    lhsT=uv_codes[:, latent].bitcast(FP8X4),
+                    lhsT_scale=uv_scales[:, latent],
+                    rhs=wo_codes[:, head].bitcast(FP8X4),
+                    rhs_scale=wo_scales[:, head],
+                    start=True,
+                    stop=True,
+                )
+            nc.vector.tensor_copy(
+                out=v_grouped[:, h * HS * PACK : (h + 1) * HS * PACK].rearrange("p (s t) -> p s t", t=PACK),
+                in_=v_acc[:].rearrange("p t s -> p s t"),
+            )
+        quantise(nc, v_grouped, v_codes, v_scales)
+
+        for step in range(1, Y_TILES + MULTIPLY_LAG):
+            if step + Y_TILES_IN_SBUF - 1 < Y_TILES:
+                load_y(step + Y_TILES_IN_SBUF - 1)
+            if step < Y_TILES:
+                transpose_y(step)
+            if step >= MULTIPLY_LAG:
+                multiply_y(step - MULTIPLY_LAG)
+            if step - 1 < Y_TILES:
+                quantise_y(step - 1)
+            if step >= MULTIPLY_LAG:
+                empty_y(step - MULTIPLY_LAG)

@@ -17,84 +17,164 @@ HALVES = WORDS // P
 
 B, NH, T, HS = 4, 4, 1024, 128
 C = NH * HS
-Y_TILES = B * NH
-ROW_TILES = T // P
+UNITS = B * NH
+ROW_TILES = 8
 PAIR = 2
-GROUPS_PER_BANK = 4
+GROUPS = 4
 
-Y_TILES_IN_SBUF = 12
-MULTIPLY_LAG = 2
+Y_IN_SBUF = 12
+LAG = 2
+NPRE = 0
+PLANE_BANKS = 4
+ACC_BANKS = 4
+SCALAR_EMPTIES = ()
+HEAD_PIECES = 4
+TOKEN_MAJOR_BATCHES = 1
+PINNED = False
+WO_FIRST = True
+MX_BUFS = 3
+GROUPED_BUFS = 3
 
 FLOPS = 2 * K * K * C + 2 * B * NH * T * K * HS
-
-
-def transpose_rows(nc, pools, identity, rows, row_tiles):
-    row_words = rows.bitcast(F32)
-    grouped = pools["grouped"].tile([P, row_tiles * P * PACK], BF16, tag="grouped", align_bytes=64)
-    grouped_words = grouped[:].bitcast(F32)
-    bank_words = PAIR * P * HALVES
-    for pair in range(row_tiles // PAIR):
-        planes = pools["planes"].tile([P, HALVES, PAIR * P], F32, tag="planes")
-        for i in range(PAIR):
-            for u in range(HALVES):
-                word = (pair * PAIR + i) * WORDS
-                nc.tensor.transpose(
-                    planes[:, u, i * P : (i + 1) * P],
-                    row_words[:, word + u : word + WORDS : HALVES],
-                    identity,
-                )
-        nc.scalar.copy(
-            out=grouped_words[:, pair * bank_words : (pair + 1) * bank_words].rearrange(
-                "p (n u) -> p n u", u=HALVES
-            ),
-            in_=planes[:].rearrange("p u n -> p n u"),
-        )
-    return grouped
-
-
-def quantise(nc, grouped, codes, scales):
-    nc.vector.quantize_mx(out=codes[:].bitcast(FP8X4), scales=scales[:], in_=grouped[:])
 
 
 def tile_causalselfattention_pc_t_kernel(tc, y_lat, W_uv, W_o, out):
     nc = tc.nc
     with ExitStack() as ctx:
         keep = ctx.enter_context(tc.tile_pool(name="keep", bufs=1))
-        y_pool = ctx.enter_context(tc.tile_pool(name="y_rows", bufs=Y_TILES_IN_SBUF))
-        out_pool = ctx.enter_context(tc.tile_pool(name="result", bufs=B))
-        mx_pool = ctx.enter_context(tc.tile_pool(name="mx", bufs=3))
-        pools = {
-            "grouped": ctx.enter_context(tc.tile_pool(name="grouped", bufs=3)),
-            "planes": ctx.enter_context(tc.psum_pool(name="planes", bufs=4)),
-        }
-        acc_pool = ctx.enter_context(tc.psum_pool(name="acc", bufs=4))
+        y_pool = ctx.enter_context(tc.tile_pool(name="y_rows", bufs=Y_IN_SBUF))
+        res_pool = ctx.enter_context(tc.tile_pool(name="result", bufs=1))
+        mx_pool = ctx.enter_context(tc.tile_pool(name="mx", bufs=MX_BUFS))
+        grouped_pool = ctx.enter_context(tc.tile_pool(name="grouped", bufs=GROUPED_BUFS))
+        pre_pool = ctx.enter_context(tc.tile_pool(name="sorted", bufs=1))
+        planes_pool = ctx.enter_context(tc.psum_pool(name="planes", bufs=PLANE_BANKS))
+        acc_pool = ctx.enter_context(tc.psum_pool(name="acc", bufs=ACC_BANKS))
+        if PINNED:
+            ctx.enter_context(tc.manual_schedule())
 
         identity = keep.tile([P, P], F32)
         make_identity(nc, identity[:])
 
+        def transpose_rows(words_of, sorted_of, row_tiles):
+            grouped = grouped_pool.tile([P, row_tiles * P * PACK], BF16, tag="grouped", align_bytes=64)
+            grouped_words = grouped[:].bitcast(F32)
+            bank_words = PAIR * P * HALVES
+            for pair in range(row_tiles // PAIR):
+                planes = planes_pool.tile([P, HALVES, PAIR * P], F32, tag="planes")
+                for i in range(PAIR):
+                    r = pair * PAIR + i
+                    for u in range(HALVES):
+                        if sorted_of(r) is None:
+                            source = words_of(r)[:, u:WORDS:HALVES]
+                        else:
+                            source = sorted_of(r)[:, u, :]
+                        nc.tensor.transpose(planes[:, u, i * P : (i + 1) * P], source, identity[:])
+                nc.scalar.copy(
+                    out=grouped_words[:, pair * bank_words : (pair + 1) * bank_words].rearrange(
+                        "p (n u) -> p n u", u=HALVES
+                    ),
+                    in_=planes[:].rearrange("p u n -> p n u"),
+                )
+            return grouped
+
+        def quantise(grouped, codes, scales):
+            nc.vector.quantize_mx(out=codes[:].bitcast(FP8X4), scales=scales[:], in_=grouped[:])
+
+        results = {}
+        units = []
+        for b in range(B - TOKEN_MAJOR_BATCHES):
+            results[(b, 0)] = res_pool.tile([P, ROW_TILES, C], F32, name="result_%d" % b)
+            out_rows = out[b].rearrange("(p i) c -> p i c", i=ROW_TILES)
+            for h in range(NH):
+                banks = []
+                for j in range(ROW_TILES // GROUPS):
+                    rows = slice(j * GROUPS, (j + 1) * GROUPS)
+                    banks.append(
+                        dict(
+                            groups=[(j * GROUPS + g, h) for g in range(GROUPS)],
+                            shape="p g s -> p g s",
+                            to=results[(b, 0)][:, rows, h * HS : (h + 1) * HS],
+                            store=(out_rows[:, rows, :], results[(b, 0)][:, rows, :]) if h == NH - 1 else None,
+                        )
+                    )
+                units.append(
+                    dict(source=y_lat[b, h].rearrange("(p i) l -> p (i l)", i=ROW_TILES), split=1, banks=banks)
+                )
+        for b in range(B - TOKEN_MAJOR_BATCHES, B):
+            for c in range(2):
+                results[(b, c)] = res_pool.tile([P, GROUPS, C], F32, name="result_%d_%d" % (b, c))
+                tokens = slice(c * GROUPS * P, (c + 1) * GROUPS * P)
+                out_rows = out[b, tokens, :].rearrange("(p i) c -> p i c", i=GROUPS)
+                for hp in range(2):
+                    banks = []
+                    for j in range(2):
+                        rows = slice(2 * j, 2 * j + 2)
+                        banks.append(
+                            dict(
+                                groups=[(hh * GROUPS + 2 * j + ii, 2 * hp + hh) for ii in range(2) for hh in range(2)],
+                                shape="p (i h) s -> p i (h s)",
+                                to=results[(b, c)][:, rows, 2 * hp * HS : 2 * (hp + 1) * HS],
+                                store=(out_rows[:, rows, :], results[(b, c)][:, rows, :]) if hp == 1 else None,
+                            )
+                        )
+                    units.append(
+                        dict(
+                            source=y_lat[b, 2 * hp : 2 * hp + 2, tokens, :].rearrange("h (p i) l -> p h (i l)", i=GROUPS),
+                            split=2,
+                            banks=banks,
+                        )
+                    )
+
         uv_rows = keep.tile([P, PACK, K], BF16)
-        nc.sync.dma_start(out=uv_rows[:], in_=W_uv.rearrange("(p t) l -> p t l", t=PACK))
         wo_rows = keep.tile([P, NH * K], BF16)
-        nc.sync.dma_start(
-            out=wo_rows[:].rearrange("p (h j) -> p h j", h=NH),
-            in_=W_o.rearrange("(h p) j -> p h j", p=P),
-        )
 
-        y_rows = {}
+        def load_uv():
+            nc.sync.dma_start(out=uv_rows[:], in_=W_uv.rearrange("(p t) l -> p t l", t=PACK))
 
-        def load_y(n):
-            y_rows[n] = y_pool.tile([P, ROW_TILES * K], BF16, name="y_rows")
+        def load_wo():
             nc.sync.dma_start(
-                out=y_rows[n][:],
-                in_=y_lat[n // NH, n % NH].rearrange("(p i) l -> p (i l)", i=ROW_TILES),
+                out=wo_rows[:].rearrange("p (h j) -> p h j", h=NH), in_=W_o.rearrange("(h p) j -> p h j", p=P)
             )
 
-        for n in range(Y_TILES_IN_SBUF):
+        if WO_FIRST:
+            load_wo()
+            load_uv()
+        else:
+            load_uv()
+            load_wo()
+
+        y_words = {}
+
+        def load_y(n):
+            unit = units[n]
+            if n == 0 and HEAD_PIECES > 1:
+                per = ROW_TILES // HEAD_PIECES
+                pieces = []
+                for q in range(HEAD_PIECES):
+                    piece = keep.tile([P, per * K], BF16, name="head_%d" % q)
+                    nc.sync.dma_start(out=piece[:], in_=unit["source"][:, q * per * K : (q + 1) * per * K])
+                    pieces.append(piece)
+                y_words[n] = [
+                    pieces[r // per][:].bitcast(F32)[:, (r % per) * WORDS : (r % per + 1) * WORDS]
+                    for r in range(ROW_TILES)
+                ]
+                return
+            rows = y_pool.tile([P, ROW_TILES * K], BF16, name="y_rows")
+            if unit["split"] == 1:
+                nc.sync.dma_start(out=rows[:], in_=unit["source"])
+            else:
+                nc.sync.dma_start(out=rows[:].rearrange("p (h x) -> p h x", h=unit["split"]), in_=unit["source"])
+            y_words[n] = [rows[:].bitcast(F32)[:, r * WORDS : (r + 1) * WORDS] for r in range(ROW_TILES)]
+            y_words[(n, "all")] = rows[:].bitcast(F32)
+
+        ahead = Y_IN_SBUF + (1 if HEAD_PIECES > 1 else 0)
+        for n in range(ahead):
             load_y(n)
 
-        wo_grouped = transpose_rows(nc, pools, identity[:], wo_rows[:], NH)
+        wo_words = wo_rows[:].bitcast(F32)
+        wo_grouped = transpose_rows(lambda r: wo_words[:, r * WORDS : (r + 1) * WORDS], lambda r: None, NH)
 
-        uv_grouped = pools["grouped"].tile([P, K * PACK], BF16, tag="grouped", align_bytes=64)
+        uv_grouped = grouped_pool.tile([P, K * PACK], BF16, tag="grouped", align_bytes=64)
         uv_by_code = uv_rows[:].rearrange("p t (m c) -> p c m t", c=PACK)
         for code in range(PACK):
             nc.vector.tensor_copy(
@@ -103,30 +183,43 @@ def tile_causalselfattention_pc_t_kernel(tc, y_lat, W_uv, W_o, out):
             )
         uv_codes = keep.tile([P, K], U32, align_bytes=64)
         uv_scales = keep.tile([P, K], U8, align_bytes=64)
-        quantise(nc, uv_grouped, uv_codes, uv_scales)
+        quantise(uv_grouped, uv_codes, uv_scales)
         wo_codes = keep.tile([P, C], U32, align_bytes=64)
         wo_scales = keep.tile([P, C], U8, align_bytes=64)
-        quantise(nc, wo_grouped, wo_codes, wo_scales)
+        quantise(wo_grouped, wo_codes, wo_scales)
 
-        y_grouped, y_codes, y_scales, y_acc, results = {}, {}, {}, {}, {}
+        y_sorted, y_grouped, y_codes, y_scales, y_acc = {}, {}, {}, {}, {}
         v_codes = keep.tile([P, C], U32, align_bytes=64)
         v_scales = keep.tile([P, C], U8, align_bytes=64)
 
+        def sort_y(n):
+            if NPRE == 0 or (n, "all") not in y_words:
+                return
+            y_sorted[n] = pre_pool.tile([P, NPRE, HALVES, P], F32, name="y_sorted")
+            nc.vector.tensor_copy(
+                out=y_sorted[n][:],
+                in_=y_words[(n, "all")][:, 0 : NPRE * WORDS].rearrange("p (r w u) -> p r u w", r=NPRE, u=HALVES),
+            )
+
         def transpose_y(n):
-            y_grouped[n] = transpose_rows(nc, pools, identity[:], y_rows[n][:], ROW_TILES)
+            y_grouped[n] = transpose_rows(
+                lambda r: y_words[n][r],
+                lambda r: y_sorted[n][:, r] if (n in y_sorted and r < NPRE) else None,
+                ROW_TILES,
+            )
 
         def quantise_y(n):
             y_codes[n] = mx_pool.tile([P, ROW_TILES * P], U32, name="y_codes", align_bytes=64)
             y_scales[n] = mx_pool.tile([P, ROW_TILES * P], U8, name="y_scales", align_bytes=64)
-            quantise(nc, y_grouped[n], y_codes[n], y_scales[n])
+            quantise(y_grouped[n], y_codes[n], y_scales[n])
 
         def multiply_y(n):
-            head = slice((n % NH) * HS, (n % NH + 1) * HS)
             y_acc[n] = []
-            for first in range(0, ROW_TILES, GROUPS_PER_BANK):
-                acc = acc_pool.tile([P, GROUPS_PER_BANK, HS], F32, tag="acc")
-                for g in range(GROUPS_PER_BANK):
-                    tokens = slice((first + g) * P, (first + g + 1) * P)
+            for bank in units[n]["banks"]:
+                acc = acc_pool.tile([P, GROUPS, HS], F32, tag="acc")
+                for g, (r, h) in enumerate(bank["groups"]):
+                    tokens = slice(r * P, (r + 1) * P)
+                    head = slice(h * HS, (h + 1) * HS)
                     nc.tensor.matmul_mx(
                         out=acc[:, g, :],
                         lhsT=y_codes[n][:, tokens].bitcast(FP8X4),
@@ -139,19 +232,19 @@ def tile_causalselfattention_pc_t_kernel(tc, y_lat, W_uv, W_o, out):
                 y_acc[n].append(acc)
 
         def empty_y(n):
-            b, h = n // NH, n % NH
-            if h == 0:
-                results[b] = out_pool.tile([P, ROW_TILES, C], F32, name="result")
-            out_rows = out[b].rearrange("(p i) c -> p i c", i=ROW_TILES)
-            for bank, acc in enumerate(y_acc[n]):
-                done = slice(bank * GROUPS_PER_BANK, (bank + 1) * GROUPS_PER_BANK)
-                nc.vector.tensor_copy(out=results[b][:, done, h * HS : (h + 1) * HS], in_=acc[:])
-                if h == NH - 1:
-                    nc.sync.dma_start(out=out_rows[:, done, :], in_=results[b][:, done, :])
+            for j, bank in enumerate(units[n]["banks"]):
+                source = y_acc[n][j][:].rearrange(bank["shape"], i=2) if "i" in bank["shape"] else y_acc[n][j][:]
+                if j in SCALAR_EMPTIES:
+                    nc.scalar.copy(out=bank["to"], in_=source)
+                else:
+                    nc.vector.tensor_copy(out=bank["to"], in_=source)
+                if bank["store"] is not None:
+                    nc.sync.dma_start(out=bank["store"][0], in_=bank["store"][1])
 
         transpose_y(0)
+        sort_y(1)
 
-        v_grouped = pools["grouped"].tile([P, C * PACK], BF16, tag="grouped", align_bytes=64)
+        v_grouped = grouped_pool.tile([P, C * PACK], BF16, tag="grouped", align_bytes=64)
         for h in range(NH):
             head = slice(h * HS, (h + 1) * HS)
             v_acc = acc_pool.tile([P, PACK, HS], F32, tag="acc")
@@ -170,16 +263,18 @@ def tile_causalselfattention_pc_t_kernel(tc, y_lat, W_uv, W_o, out):
                 out=v_grouped[:, h * HS * PACK : (h + 1) * HS * PACK].rearrange("p (s t) -> p s t", t=PACK),
                 in_=v_acc[:].rearrange("p t s -> p s t"),
             )
-        quantise(nc, v_grouped, v_codes, v_scales)
+        quantise(v_grouped, v_codes, v_scales)
 
-        for step in range(1, Y_TILES + MULTIPLY_LAG):
-            if step + Y_TILES_IN_SBUF - 1 < Y_TILES:
-                load_y(step + Y_TILES_IN_SBUF - 1)
-            if step < Y_TILES:
+        for step in range(1, UNITS + LAG):
+            if step + ahead - 1 < UNITS:
+                load_y(step + ahead - 1)
+            if step + 1 < UNITS:
+                sort_y(step + 1)
+            if step < UNITS:
                 transpose_y(step)
-            if step >= MULTIPLY_LAG:
-                multiply_y(step - MULTIPLY_LAG)
-            if step - 1 < Y_TILES:
+            if step >= LAG:
+                multiply_y(step - LAG)
+            if step - 1 < UNITS:
                 quantise_y(step - 1)
-            if step >= MULTIPLY_LAG:
-                empty_y(step - MULTIPLY_LAG)
+            if step >= LAG:
+                empty_y(step - LAG)

@@ -24,7 +24,7 @@ GROUPS = 4
 
 Y_IN_SBUF = 12
 LAG = 2
-NPRE = 0
+NPRE = 4
 PLANE_BANKS = 4
 ACC_BANKS = 4
 SCALAR_EMPTIES = ()
@@ -46,7 +46,7 @@ def tile_causalselfattention_pc_t_kernel(tc, y_lat, W_uv, W_o, out):
         res_pool = ctx.enter_context(tc.tile_pool(name="result", bufs=1))
         mx_pool = ctx.enter_context(tc.tile_pool(name="mx", bufs=MX_BUFS))
         grouped_pool = ctx.enter_context(tc.tile_pool(name="grouped", bufs=GROUPED_BUFS))
-        pre_pool = ctx.enter_context(tc.tile_pool(name="sorted", bufs=1))
+        pre_pool = ctx.enter_context(tc.tile_pool(name="sorted", bufs=2))
         planes_pool = ctx.enter_context(tc.psum_pool(name="planes", bufs=PLANE_BANKS))
         acc_pool = ctx.enter_context(tc.psum_pool(name="acc", bufs=ACC_BANKS))
         if PINNED:
@@ -196,7 +196,7 @@ def tile_causalselfattention_pc_t_kernel(tc, y_lat, W_uv, W_o, out):
             if NPRE == 0 or (n, "all") not in y_words:
                 return
             y_sorted[n] = pre_pool.tile([P, NPRE, HALVES, P], F32, name="y_sorted")
-            nc.vector.tensor_copy(
+            nc.gpsimd.tensor_copy(
                 out=y_sorted[n][:],
                 in_=y_words[(n, "all")][:, 0 : NPRE * WORDS].rearrange("p (r w u) -> p r u w", r=NPRE, u=HALVES),
             )

@@ -22,18 +22,14 @@ ROW_TILES = 8
 PAIR = 2
 GROUPS = 4
 
-Y_IN_SBUF = 12
 LAG = 2
 NPRE = 4
+FIRST_SORTED = 3
+SORT_PIECES = 1
 PLANE_BANKS = 4
 ACC_BANKS = 4
-SCALAR_EMPTIES = ()
 HEAD_PIECES = 4
-TOKEN_MAJOR_BATCHES = 1
-PINNED = False
-WO_FIRST = True
-MX_BUFS = 3
-GROUPED_BUFS = 3
+FINE_UNITS = 0
 
 FLOPS = 2 * K * K * C + 2 * B * NH * T * K * HS
 
@@ -42,32 +38,27 @@ def tile_causalselfattention_pc_t_kernel(tc, y_lat, W_uv, W_o, out):
     nc = tc.nc
     with ExitStack() as ctx:
         keep = ctx.enter_context(tc.tile_pool(name="keep", bufs=1))
-        y_pool = ctx.enter_context(tc.tile_pool(name="y_rows", bufs=Y_IN_SBUF))
+        y_pool = ctx.enter_context(tc.tile_pool(name="y_rows", bufs=12))
+        pair_pool = ctx.enter_context(tc.tile_pool(name="y_pairs", bufs=1))
         res_pool = ctx.enter_context(tc.tile_pool(name="result", bufs=1))
-        mx_pool = ctx.enter_context(tc.tile_pool(name="mx", bufs=MX_BUFS))
-        grouped_pool = ctx.enter_context(tc.tile_pool(name="grouped", bufs=GROUPED_BUFS))
+        mx_pool = ctx.enter_context(tc.tile_pool(name="mx", bufs=3))
+        grouped_pool = ctx.enter_context(tc.tile_pool(name="grouped", bufs=3))
         pre_pool = ctx.enter_context(tc.tile_pool(name="sorted", bufs=2))
         planes_pool = ctx.enter_context(tc.psum_pool(name="planes", bufs=PLANE_BANKS))
         acc_pool = ctx.enter_context(tc.psum_pool(name="acc", bufs=ACC_BANKS))
-        if PINNED:
-            ctx.enter_context(tc.manual_schedule())
 
         identity = keep.tile([P, P], F32)
         make_identity(nc, identity[:])
 
-        def transpose_rows(words_of, sorted_of, row_tiles):
-            grouped = grouped_pool.tile([P, row_tiles * P * PACK], BF16, tag="grouped", align_bytes=64)
-            grouped_words = grouped[:].bitcast(F32)
+        def transpose_rows(sources, grouped):
+            grouped_words = grouped.bitcast(F32)
             bank_words = PAIR * P * HALVES
-            for pair in range(row_tiles // PAIR):
+            for pair in range(len(sources) // PAIR):
                 planes = planes_pool.tile([P, HALVES, PAIR * P], F32, tag="planes")
                 for i in range(PAIR):
-                    r = pair * PAIR + i
+                    words, is_sorted = sources[pair * PAIR + i]
                     for u in range(HALVES):
-                        if sorted_of(r) is None:
-                            source = words_of(r)[:, u:WORDS:HALVES]
-                        else:
-                            source = sorted_of(r)[:, u, :]
+                        source = words[:, u, :] if is_sorted else words[:, u:WORDS:HALVES]
                         nc.tensor.transpose(planes[:, u, i * P : (i + 1) * P], source, identity[:])
                 nc.scalar.copy(
                     out=grouped_words[:, pair * bank_words : (pair + 1) * bank_words].rearrange(
@@ -75,150 +66,170 @@ def tile_causalselfattention_pc_t_kernel(tc, y_lat, W_uv, W_o, out):
                     ),
                     in_=planes[:].rearrange("p u n -> p n u"),
                 )
-            return grouped
 
         def quantise(grouped, codes, scales):
-            nc.vector.quantize_mx(out=codes[:].bitcast(FP8X4), scales=scales[:], in_=grouped[:])
+            nc.vector.quantize_mx(out=codes.bitcast(FP8X4), scales=scales, in_=grouped)
 
-        results = {}
         units = []
-        for b in range(B - TOKEN_MAJOR_BATCHES):
-            results[(b, 0)] = res_pool.tile([P, ROW_TILES, C], F32, name="result_%d" % b)
+        for b in range(B - 1):
+            result = res_pool.tile([P, ROW_TILES, C], F32, name="result_%d" % b)
             out_rows = out[b].rearrange("(p i) c -> p i c", i=ROW_TILES)
             for h in range(NH):
                 banks = []
                 for j in range(ROW_TILES // GROUPS):
                     rows = slice(j * GROUPS, (j + 1) * GROUPS)
+                    then_store = None
+                    if h == NH - 1:
+                        then_store = (out_rows[:, rows, :], result[:, rows, :])
+                    banks.append(
+                        dict(slots=list(range(j * GROUPS, (j + 1) * GROUPS)), to=result[:, rows, h * HS : (h + 1) * HS], store=then_store)
+                    )
+                units.append(dict(rows=[(r, h) for r in range(ROW_TILES)], banks=banks, parts=1))
+        for c in range(2):
+            result = res_pool.tile([P, GROUPS, C], F32, name="result_3_%d" % c)
+            tokens = slice(c * GROUPS * P, (c + 1) * GROUPS * P)
+            out_rows = out[B - 1, tokens, :].rearrange("(p i) c -> p i c", i=GROUPS)
+            for hp in range(2):
+                n = len(units)
+                fine = n >= UNITS - FINE_UNITS
+                per = 1 if fine else 2
+                columns = slice(2 * hp * HS, 2 * (hp + 1) * HS)
+                banks = []
+                for j in range(GROUPS // per):
+                    rows = slice(per * j, per * (j + 1))
                     banks.append(
                         dict(
-                            groups=[(j * GROUPS + g, h) for g in range(GROUPS)],
-                            shape="p g s -> p g s",
-                            to=results[(b, 0)][:, rows, h * HS : (h + 1) * HS],
-                            store=(out_rows[:, rows, :], results[(b, 0)][:, rows, :]) if h == NH - 1 else None,
+                            slots=list(range(2 * per * j, 2 * per * (j + 1))),
+                            to=result[:, rows, columns],
+                            store=(out_rows[:, rows, :], result[:, rows, :]) if hp == 1 else None,
                         )
                     )
                 units.append(
-                    dict(source=y_lat[b, h].rearrange("(p i) l -> p (i l)", i=ROW_TILES), split=1, banks=banks)
-                )
-        for b in range(B - TOKEN_MAJOR_BATCHES, B):
-            for c in range(2):
-                results[(b, c)] = res_pool.tile([P, GROUPS, C], F32, name="result_%d_%d" % (b, c))
-                tokens = slice(c * GROUPS * P, (c + 1) * GROUPS * P)
-                out_rows = out[b, tokens, :].rearrange("(p i) c -> p i c", i=GROUPS)
-                for hp in range(2):
-                    banks = []
-                    for j in range(2):
-                        rows = slice(2 * j, 2 * j + 2)
-                        banks.append(
-                            dict(
-                                groups=[(hh * GROUPS + 2 * j + ii, 2 * hp + hh) for ii in range(2) for hh in range(2)],
-                                shape="p (i h) s -> p i (h s)",
-                                to=results[(b, c)][:, rows, 2 * hp * HS : 2 * (hp + 1) * HS],
-                                store=(out_rows[:, rows, :], results[(b, c)][:, rows, :]) if hp == 1 else None,
-                            )
-                        )
-                    units.append(
-                        dict(
-                            source=y_lat[b, 2 * hp : 2 * hp + 2, tokens, :].rearrange("h (p i) l -> p h (i l)", i=GROUPS),
-                            split=2,
-                            banks=banks,
-                        )
+                    dict(
+                        rows=[(e * GROUPS + i, 2 * hp + e) for i in range(GROUPS) for e in range(2)],
+                        banks=banks,
+                        parts=GROUPS if fine else 1,
                     )
+                )
 
         uv_rows = keep.tile([P, PACK, K], BF16)
         wo_rows = keep.tile([P, NH * K], BF16)
-
-        def load_uv():
-            nc.sync.dma_start(out=uv_rows[:], in_=W_uv.rearrange("(p t) l -> p t l", t=PACK))
-
-        def load_wo():
-            nc.sync.dma_start(
-                out=wo_rows[:].rearrange("p (h j) -> p h j", h=NH), in_=W_o.rearrange("(h p) j -> p h j", p=P)
-            )
-
-        if WO_FIRST:
-            load_wo()
-            load_uv()
-        else:
-            load_uv()
-            load_wo()
+        nc.sync.dma_start(out=wo_rows[:].rearrange("p (h j) -> p h j", h=NH), in_=W_o.rearrange("(h p) j -> p h j", p=P))
+        nc.sync.dma_start(out=uv_rows[:], in_=W_uv.rearrange("(p t) l -> p t l", t=PACK))
 
         y_words = {}
+        load_groups = [[n] for n in range(UNITS)]
+        loaded = []
+        held_stores = []
 
-        def load_y(n):
-            unit = units[n]
-            if n == 0 and HEAD_PIECES > 1:
+        def source_of(first, count):
+            if first < UNITS - NH:
+                b, h = first // NH, first % NH
+                return count, y_lat[b, h : h + count].rearrange("h (p i) l -> p h (i l)", i=ROW_TILES)
+            c, hp = (first % NH) // 2, first % 2
+            tokens = slice(c * GROUPS * P, (c + 1) * GROUPS * P)
+            heads = slice(2 * hp, 2 * hp + 2 * count)
+            return 2 * count, y_lat[B - 1, heads, tokens, :].rearrange("h (p i) l -> p h (i l)", i=GROUPS)
+
+        def load_next():
+            members = load_groups[len(loaded)]
+            loaded.append(members)
+            first = members[0]
+            runs, source = source_of(first, len(members))
+            if first == 0 and HEAD_PIECES > 1:
                 per = ROW_TILES // HEAD_PIECES
                 pieces = []
                 for q in range(HEAD_PIECES):
                     piece = keep.tile([P, per * K], BF16, name="head_%d" % q)
-                    nc.sync.dma_start(out=piece[:], in_=unit["source"][:, q * per * K : (q + 1) * per * K])
-                    pieces.append(piece)
-                y_words[n] = [
-                    pieces[r // per][:].bitcast(F32)[:, (r % per) * WORDS : (r % per + 1) * WORDS]
-                    for r in range(ROW_TILES)
-                ]
+                    nc.sync.dma_start(out=piece[:], in_=source[:, 0, q * per * K : (q + 1) * per * K])
+                    pieces.append(piece[:].bitcast(F32))
+                y_words[0] = [pieces[r // per][:, (r % per) * WORDS : (r % per + 1) * WORDS] for r in range(ROW_TILES)]
                 return
-            rows = y_pool.tile([P, ROW_TILES * K], BF16, name="y_rows")
-            if unit["split"] == 1:
-                nc.sync.dma_start(out=rows[:], in_=unit["source"])
+            if len(members) == 1:
+                rows = y_pool.tile([P, ROW_TILES * K], BF16, name="y_rows")
             else:
-                nc.sync.dma_start(out=rows[:].rearrange("p (h x) -> p h x", h=unit["split"]), in_=unit["source"])
-            y_words[n] = [rows[:].bitcast(F32)[:, r * WORDS : (r + 1) * WORDS] for r in range(ROW_TILES)]
-            y_words[(n, "all")] = rows[:].bitcast(F32)
+                rows = pair_pool.tile([P, len(members) * ROW_TILES * K], BF16, name="y_pair")
+            nc.sync.dma_start(out=rows[:].rearrange("p (h x) -> p h x", h=runs), in_=source)
+            words = rows[:].bitcast(F32)
+            for k, n in enumerate(members):
+                base = k * ROW_TILES * WORDS
+                y_words[n] = [words[:, base + r * WORDS : base + (r + 1) * WORDS] for r in range(ROW_TILES)]
+                y_words[(n, "all")] = words[:, base : base + ROW_TILES * WORDS]
 
-        ahead = Y_IN_SBUF + (1 if HEAD_PIECES > 1 else 0)
-        for n in range(ahead):
-            load_y(n)
+        def store_rows(pair_of_views):
+            if False:
+                held_stores.append(pair_of_views)
+                return
+            nc.sync.dma_start(out=pair_of_views[0], in_=pair_of_views[1])
+
+        for first_loads in range(13):
+            load_next()
 
         wo_words = wo_rows[:].bitcast(F32)
-        wo_grouped = transpose_rows(lambda r: wo_words[:, r * WORDS : (r + 1) * WORDS], lambda r: None, NH)
+        wo_grouped = grouped_pool.tile([P, NH * P * PACK], BF16, tag="grouped", align_bytes=64)
+        transpose_rows([(wo_words[:, r * WORDS : (r + 1) * WORDS], False) for r in range(NH)], wo_grouped[:])
 
         uv_grouped = grouped_pool.tile([P, K * PACK], BF16, tag="grouped", align_bytes=64)
         uv_by_code = uv_rows[:].rearrange("p t (m c) -> p c m t", c=PACK)
         for code in range(PACK):
-            nc.vector.tensor_copy(
-                out=uv_grouped[:, code * K : (code + 1) * K].rearrange("p (m t) -> p m t", t=PACK),
-                in_=uv_by_code[:, code],
-            )
+            to = uv_grouped[:, code * K : (code + 1) * K].rearrange("p (m t) -> p m t", t=PACK)
+            if code in ():
+                nc.scalar.copy(out=to, in_=uv_by_code[:, code])
+            else:
+                nc.vector.tensor_copy(out=to, in_=uv_by_code[:, code])
         uv_codes = keep.tile([P, K], U32, align_bytes=64)
         uv_scales = keep.tile([P, K], U8, align_bytes=64)
-        quantise(uv_grouped, uv_codes, uv_scales)
+        quantise(uv_grouped[:], uv_codes[:], uv_scales[:])
         wo_codes = keep.tile([P, C], U32, align_bytes=64)
         wo_scales = keep.tile([P, C], U8, align_bytes=64)
-        quantise(wo_grouped, wo_codes, wo_scales)
+        quantise(wo_grouped[:], wo_codes[:], wo_scales[:])
 
         y_sorted, y_grouped, y_codes, y_scales, y_acc = {}, {}, {}, {}, {}
         v_codes = keep.tile([P, C], U32, align_bytes=64)
         v_scales = keep.tile([P, C], U8, align_bytes=64)
 
         def sort_y(n):
-            if NPRE == 0 or (n, "all") not in y_words:
+            if NPRE == 0 or n < FIRST_SORTED:
                 return
+            first_word = (ROW_TILES - NPRE) * WORDS
             y_sorted[n] = pre_pool.tile([P, NPRE, HALVES, P], F32, name="y_sorted")
-            nc.gpsimd.tensor_copy(
-                out=y_sorted[n][:],
-                in_=y_words[(n, "all")][:, 0 : NPRE * WORDS].rearrange("p (r w u) -> p r u w", r=NPRE, u=HALVES),
-            )
+            per = NPRE // SORT_PIECES
+            for q in range(SORT_PIECES):
+                nc.gpsimd.tensor_copy(
+                    out=y_sorted[n][:, q * per : (q + 1) * per],
+                    in_=y_words[(n, "all")][:, first_word + q * per * WORDS : first_word + (q + 1) * per * WORDS].rearrange(
+                        "p (r w u) -> p r u w", r=per, u=HALVES
+                    ),
+                )
 
         def transpose_y(n):
-            y_grouped[n] = transpose_rows(
-                lambda r: y_words[n][r],
-                lambda r: y_sorted[n][:, r] if (n in y_sorted and r < NPRE) else None,
-                ROW_TILES,
-            )
+            y_grouped[n] = grouped_pool.tile([P, ROW_TILES * P * PACK], BF16, name="grouped", tag="grouped", align_bytes=64)
+            sources = []
+            for r, h in units[n]["rows"]:
+                if n in y_sorted and r >= ROW_TILES - NPRE:
+                    sources.append((y_sorted[n][:, r - (ROW_TILES - NPRE)], True))
+                else:
+                    sources.append((y_words[n][r], False))
+            transpose_rows(sources, y_grouped[n][:])
 
         def quantise_y(n):
             y_codes[n] = mx_pool.tile([P, ROW_TILES * P], U32, name="y_codes", align_bytes=64)
             y_scales[n] = mx_pool.tile([P, ROW_TILES * P], U8, name="y_scales", align_bytes=64)
-            quantise(y_grouped[n], y_codes[n], y_scales[n])
+            parts = units[n]["parts"]
+            width = ROW_TILES * P // parts
+            for q in range(parts):
+                columns = slice(q * width, (q + 1) * width)
+                quantise(
+                    y_grouped[n][:, q * width * PACK : (q + 1) * width * PACK], y_codes[n][:, columns], y_scales[n][:, columns]
+                )
 
         def multiply_y(n):
             y_acc[n] = []
             for bank in units[n]["banks"]:
-                acc = acc_pool.tile([P, GROUPS, HS], F32, tag="acc")
-                for g, (r, h) in enumerate(bank["groups"]):
-                    tokens = slice(r * P, (r + 1) * P)
+                acc = acc_pool.tile([P, len(bank["slots"]), HS], F32, tag="acc")
+                for g, s in enumerate(bank["slots"]):
+                    h = units[n]["rows"][s][1]
+                    tokens = slice(s * P, (s + 1) * P)
                     head = slice(h * HS, (h + 1) * HS)
                     nc.tensor.matmul_mx(
                         out=acc[:, g, :],
@@ -233,13 +244,14 @@ def tile_causalselfattention_pc_t_kernel(tc, y_lat, W_uv, W_o, out):
 
         def empty_y(n):
             for j, bank in enumerate(units[n]["banks"]):
-                source = y_acc[n][j][:].rearrange(bank["shape"], i=2) if "i" in bank["shape"] else y_acc[n][j][:]
-                if j in SCALAR_EMPTIES:
+                rows_of_out = bank["to"].shape[1]
+                source = y_acc[n][j][:].rearrange("p (i e) s -> p i (e s)", i=rows_of_out)
+                if False:
                     nc.scalar.copy(out=bank["to"], in_=source)
                 else:
                     nc.vector.tensor_copy(out=bank["to"], in_=source)
                 if bank["store"] is not None:
-                    nc.sync.dma_start(out=bank["store"][0], in_=bank["store"][1])
+                    store_rows(bank["store"])
 
         transpose_y(0)
         sort_y(1)
@@ -259,15 +271,19 @@ def tile_causalselfattention_pc_t_kernel(tc, y_lat, W_uv, W_o, out):
                     start=True,
                     stop=True,
                 )
-            nc.vector.tensor_copy(
-                out=v_grouped[:, h * HS * PACK : (h + 1) * HS * PACK].rearrange("p (s t) -> p s t", t=PACK),
-                in_=v_acc[:].rearrange("p t s -> p s t"),
-            )
-        quantise(v_grouped, v_codes, v_scales)
+            to = v_grouped[:, h * HS * PACK : (h + 1) * HS * PACK].rearrange("p (s t) -> p s t", t=PACK)
+            if h in ():
+                nc.scalar.copy(out=to, in_=v_acc[:].rearrange("p t s -> p s t"))
+            else:
+                nc.vector.tensor_copy(out=to, in_=v_acc[:].rearrange("p t s -> p s t"))
+        quantise(v_grouped[:], v_codes[:], v_scales[:])
 
         for step in range(1, UNITS + LAG):
-            if step + ahead - 1 < UNITS:
-                load_y(step + ahead - 1)
+            while len(loaded) < len(load_groups) and len(loaded) < step + 13:
+                load_next()
+                if len(loaded) == len(load_groups):
+                    for held in held_stores:
+                        nc.sync.dma_start(out=held[0], in_=held[1])
             if step + 1 < UNITS:
                 sort_y(step + 1)
             if step < UNITS:

@@ -38,14 +38,15 @@ def tile_causalselfattention_pc_t_kernel(tc, y_lat, W_uv, W_o, out):
     nc = tc.nc
     with ExitStack() as ctx:
         keep = ctx.enter_context(tc.tile_pool(name="keep", bufs=1))
-        y_pool = ctx.enter_context(tc.tile_pool(name="y_rows", bufs=12))
-        pair_pool = ctx.enter_context(tc.tile_pool(name="y_pairs", bufs=1))
+        y_pool = ctx.enter_context(tc.tile_pool(name="y_rows", bufs=5))
+        pair_pool = ctx.enter_context(tc.tile_pool(name="y_pairs", bufs=4))
         res_pool = ctx.enter_context(tc.tile_pool(name="result", bufs=1))
         mx_pool = ctx.enter_context(tc.tile_pool(name="mx", bufs=3))
         grouped_pool = ctx.enter_context(tc.tile_pool(name="grouped", bufs=3))
         pre_pool = ctx.enter_context(tc.tile_pool(name="sorted", bufs=2))
         planes_pool = ctx.enter_context(tc.psum_pool(name="planes", bufs=PLANE_BANKS))
         acc_pool = ctx.enter_context(tc.psum_pool(name="acc", bufs=ACC_BANKS))
+        ctx.enter_context(tc.manual_schedule(engines={mybir.EngineType.SP}))
 
         identity = keep.tile([P, P], F32)
         make_identity(nc, identity[:])
@@ -80,7 +81,7 @@ def tile_causalselfattention_pc_t_kernel(tc, y_lat, W_uv, W_o, out):
                     rows = slice(j * GROUPS, (j + 1) * GROUPS)
                     then_store = None
                     if h == NH - 1:
-                        then_store = (out_rows[:, rows, :], result[:, rows, :])
+                        then_store = (out_rows, result[:]) if j == 1 else None
                     banks.append(
                         dict(slots=list(range(j * GROUPS, (j + 1) * GROUPS)), to=result[:, rows, h * HS : (h + 1) * HS], store=then_store)
                     )
@@ -101,7 +102,15 @@ def tile_causalselfattention_pc_t_kernel(tc, y_lat, W_uv, W_o, out):
                         dict(
                             slots=list(range(2 * per * j, 2 * per * (j + 1))),
                             to=result[:, rows, columns],
-                            store=(out_rows[:, rows, :], result[:, rows, :]) if hp == 1 else None,
+                            store=(
+                                None
+                                if hp == 0
+                                else (out_rows[:, rows, :], result[:, rows, :])
+                                if c == 1
+                                else (out_rows, result[:])
+                                if j == GROUPS // per - 1
+                                else None
+                            ),
                         )
                     )
                 units.append(
@@ -112,13 +121,13 @@ def tile_causalselfattention_pc_t_kernel(tc, y_lat, W_uv, W_o, out):
                     )
                 )
 
-        uv_rows = keep.tile([P, PACK, K], BF16)
-        wo_rows = keep.tile([P, NH * K], BF16)
+        wo_rows = y_pool.tile([P, NH * K], BF16, name="y_rows")
+        uv_rows = y_pool.tile([P, PACK, K], BF16, name="y_rows")
         nc.sync.dma_start(out=wo_rows[:].rearrange("p (h j) -> p h j", h=NH), in_=W_o.rearrange("(h p) j -> p h j", p=P))
         nc.sync.dma_start(out=uv_rows[:], in_=W_uv.rearrange("(p t) l -> p t l", t=PACK))
 
         y_words = {}
-        load_groups = [[n] for n in range(UNITS)]
+        load_groups = [[n] for n in range(8)] + [[n, n + 1] for n in range(8, UNITS, 2)]
         loaded = []
         held_stores = []
 
@@ -162,7 +171,7 @@ def tile_causalselfattention_pc_t_kernel(tc, y_lat, W_uv, W_o, out):
                 return
             nc.sync.dma_start(out=pair_of_views[0], in_=pair_of_views[1])
 
-        for first_loads in range(13):
+        for first_loads in range(12):
             load_next()
 
         wo_words = wo_rows[:].bitcast(F32)
@@ -279,7 +288,7 @@ def tile_causalselfattention_pc_t_kernel(tc, y_lat, W_uv, W_o, out):
         quantise(v_grouped[:], v_codes[:], v_scales[:])
 
         for step in range(1, UNITS + LAG):
-            while len(loaded) < len(load_groups) and len(loaded) < step + 13:
+            while len(loaded) < len(load_groups) and False:
                 load_next()
                 if len(loaded) == len(load_groups):
                     for held in held_stores:

@@ -23,7 +23,7 @@ PAIR = 2
 GROUPS = 4
 
 LAG = 2
-NPRE = 4
+NPRE = 3
 FIRST_SORTED = 3
 SORT_PIECES = 1
 PLANE_BANKS = 4

@@ -46,7 +46,7 @@ def tile_causalselfattention_pc_t_kernel(tc, y_lat, W_uv, W_o, out):
         pre_pool = ctx.enter_context(tc.tile_pool(name="sorted", bufs=2))
         planes_pool = ctx.enter_context(tc.psum_pool(name="planes", bufs=PLANE_BANKS))
         acc_pool = ctx.enter_context(tc.psum_pool(name="acc", bufs=ACC_BANKS))
-        ctx.enter_context(tc.manual_schedule(engines={mybir.EngineType.SP}))
+        ctx.enter_context(tc.manual_schedule())
 
         identity = keep.tile([P, P], F32)
         make_identity(nc, identity[:])

@@ -28,7 +28,7 @@ FIRST_SORTED = 3
 SORT_PIECES = 1
 PLANE_BANKS = 4
 ACC_BANKS = 4
-HEAD_PIECES = 4
+HEAD_PIECES = 1
 FINE_UNITS = 0
 
 FLOPS = 2 * K * K * C + 2 * B * NH * T * K * HS
@@ -105,8 +105,6 @@ def tile_causalselfattention_pc_t_kernel(tc, y_lat, W_uv, W_o, out):
                             store=(
                                 None
                                 if hp == 0
-                                else (out_rows[:, rows, :], result[:, rows, :])
-                                if c == 1
                                 else (out_rows, result[:])
                                 if j == GROUPS // per - 1
                                 else None

@@ -25,11 +25,6 @@ GROUPS = 4
 LAG = 2
 NPRE = 3
 FIRST_SORTED = 3
-SORT_PIECES = 1
-PLANE_BANKS = 4
-ACC_BANKS = 4
-HEAD_PIECES = 1
-FINE_UNITS = 0
 
 FLOPS = 2 * K * K * C + 2 * B * NH * T * K * HS
 
@@ -44,8 +39,8 @@ def tile_causalselfattention_pc_t_kernel(tc, y_lat, W_uv, W_o, out):
         mx_pool = ctx.enter_context(tc.tile_pool(name="mx", bufs=3))
         grouped_pool = ctx.enter_context(tc.tile_pool(name="grouped", bufs=3))
         pre_pool = ctx.enter_context(tc.tile_pool(name="sorted", bufs=2))
-        planes_pool = ctx.enter_context(tc.psum_pool(name="planes", bufs=PLANE_BANKS))
-        acc_pool = ctx.enter_context(tc.psum_pool(name="acc", bufs=ACC_BANKS))
+        planes_pool = ctx.enter_context(tc.psum_pool(name="planes", bufs=4))
+        acc_pool = ctx.enter_context(tc.psum_pool(name="acc", bufs=4))
         ctx.enter_context(tc.manual_schedule())
 
         identity = keep.tile([P, P], F32)
@@ -72,118 +67,53 @@ def tile_causalselfattention_pc_t_kernel(tc, y_lat, W_uv, W_o, out):
             nc.vector.quantize_mx(out=codes.bitcast(FP8X4), scales=scales, in_=grouped)
 
         units = []
-        for b in range(B - 1):
+        results = []
+        for b in range(B):
             result = res_pool.tile([P, ROW_TILES, C], F32, name="result_%d" % b)
-            out_rows = out[b].rearrange("(p i) c -> p i c", i=ROW_TILES)
-            for h in range(NH):
-                banks = []
-                for j in range(ROW_TILES // GROUPS):
-                    rows = slice(j * GROUPS, (j + 1) * GROUPS)
-                    then_store = None
-                    if h == NH - 1:
-                        then_store = (out_rows, result[:]) if j == 1 else None
-                    banks.append(
-                        dict(slots=list(range(j * GROUPS, (j + 1) * GROUPS)), to=result[:, rows, h * HS : (h + 1) * HS], store=then_store)
-                    )
-                units.append(dict(rows=[(r, h) for r in range(ROW_TILES)], banks=banks, parts=1))
-        for c in range(2):
-            result = res_pool.tile([P, GROUPS, C], F32, name="result_3_%d" % c)
-            tokens = slice(c * GROUPS * P, (c + 1) * GROUPS * P)
-            out_rows = out[B - 1, tokens, :].rearrange("(p i) c -> p i c", i=GROUPS)
-            for hp in range(2):
-                n = len(units)
-                fine = n >= UNITS - FINE_UNITS
-                per = 1 if fine else 2
-                columns = slice(2 * hp * HS, 2 * (hp + 1) * HS)
-                banks = []
-                for j in range(GROUPS // per):
-                    rows = slice(per * j, per * (j + 1))
-                    banks.append(
-                        dict(
-                            slots=list(range(2 * per * j, 2 * per * (j + 1))),
-                            to=result[:, rows, columns],
-                            store=(
-                                None
-                                if hp == 0
-                                else (out_rows, result[:])
-                                if j == GROUPS // per - 1
-                                else None
-                            ),
-                        )
-                    )
-                units.append(
-                    dict(
-                        rows=[(e * GROUPS + i, 2 * hp + e) for i in range(GROUPS) for e in range(2)],
-                        banks=banks,
-                        parts=GROUPS if fine else 1,
-                    )
-                )
+            results.append(result)
+            if b < B - 1:
+                units += [dict(b=b, tiles=[(h, j) for j in range(ROW_TILES)], store=None) for h in range(NH)]
+                units[-1]["store"] = range(ROW_TILES)
+            else:
+                for js in (range(0, GROUPS), range(GROUPS, ROW_TILES)):
+                    units += [dict(b=b, tiles=[(h + e, j) for e in range(2) for j in js], store=None) for h in (0, 2)]
+                    units[-1]["store"] = js
 
         wo_rows = y_pool.tile([P, NH * K], BF16, name="y_rows")
         uv_rows = y_pool.tile([P, PACK, K], BF16, name="y_rows")
-        nc.sync.dma_start(out=wo_rows[:].rearrange("p (h j) -> p h j", h=NH), in_=W_o.rearrange("(h p) j -> p h j", p=P))
+        nc.sync.dma_start(out=wo_rows[:], in_=W_o.rearrange("(n i) j -> n (i j)", i=NH))
         nc.sync.dma_start(out=uv_rows[:], in_=W_uv.rearrange("(p t) l -> p t l", t=PACK))
 
         y_words = {}
-        load_groups = [[n] for n in range(8)] + [[n, n + 1] for n in range(8, UNITS, 2)]
-        loaded = []
-        held_stores = []
-
-        def source_of(first, count):
-            if first < UNITS - NH:
-                b, h = first // NH, first % NH
-                return count, y_lat[b, h : h + count].rearrange("h (p i) l -> p h (i l)", i=ROW_TILES)
-            c, hp = (first % NH) // 2, first % 2
-            tokens = slice(c * GROUPS * P, (c + 1) * GROUPS * P)
-            heads = slice(2 * hp, 2 * hp + 2 * count)
-            return 2 * count, y_lat[B - 1, heads, tokens, :].rearrange("h (p i) l -> p h (i l)", i=GROUPS)
-
-        def load_next():
-            members = load_groups[len(loaded)]
-            loaded.append(members)
-            first = members[0]
-            runs, source = source_of(first, len(members))
-            if first == 0 and HEAD_PIECES > 1:
-                per = ROW_TILES // HEAD_PIECES
-                pieces = []
-                for q in range(HEAD_PIECES):
-                    piece = keep.tile([P, per * K], BF16, name="head_%d" % q)
-                    nc.sync.dma_start(out=piece[:], in_=source[:, 0, q * per * K : (q + 1) * per * K])
-                    pieces.append(piece[:].bitcast(F32))
-                y_words[0] = [pieces[r // per][:, (r % per) * WORDS : (r % per + 1) * WORDS] for r in range(ROW_TILES)]
-                return
-            if len(members) == 1:
-                rows = y_pool.tile([P, ROW_TILES * K], BF16, name="y_rows")
-            else:
-                rows = pair_pool.tile([P, len(members) * ROW_TILES * K], BF16, name="y_pair")
-            nc.sync.dma_start(out=rows[:].rearrange("p (h x) -> p h x", h=runs), in_=source)
+        for first in list(range(2 * NH)) + list(range(2 * NH, UNITS, 2)):
+            b, h = first // NH, first % NH
+            heads = 1 if b < 2 else 2
+            pool = y_pool if heads == 1 else pair_pool
+            rows = pool.tile([P, heads * ROW_TILES * K], BF16, name="y_rows")
+            nc.sync.dma_start(
+                out=rows[:].rearrange("p (h x) -> p h x", h=heads),
+                in_=y_lat[b, h : h + heads].rearrange("h (p j) l -> p h (j l)", j=ROW_TILES),
+            )
             words = rows[:].bitcast(F32)
-            for k, n in enumerate(members):
-                base = k * ROW_TILES * WORDS
-                y_words[n] = [words[:, base + r * WORDS : base + (r + 1) * WORDS] for r in range(ROW_TILES)]
-                y_words[(n, "all")] = words[:, base : base + ROW_TILES * WORDS]
-
-        def store_rows(pair_of_views):
-            if False:
-                held_stores.append(pair_of_views)
-                return
-            nc.sync.dma_start(out=pair_of_views[0], in_=pair_of_views[1])
-
-        for first_loads in range(12):
-            load_next()
+            for k in range(heads):
+                y_words[b, h + k] = words[:, k * ROW_TILES * WORDS : (k + 1) * ROW_TILES * WORDS]
 
         wo_words = wo_rows[:].bitcast(F32)
         wo_grouped = grouped_pool.tile([P, NH * P * PACK], BF16, tag="grouped", align_bytes=64)
-        transpose_rows([(wo_words[:, r * WORDS : (r + 1) * WORDS], False) for r in range(NH)], wo_grouped[:])
+        wo_pairs = wo_grouped[:].bitcast(F32).rearrange("p (n k x) -> p k n x", k=NH // PAIR, x=PAIR * HALVES)
+        for k in range(NH // PAIR):
+            planes = planes_pool.tile([P, PAIR * HALVES, P], F32, tag="planes")
+            for e in range(PAIR):
+                row = wo_words[:, (PAIR * k + e) * WORDS : (PAIR * k + e + 1) * WORDS]
+                for u in range(HALVES):
+                    nc.tensor.transpose(planes[:, HALVES * e + u, :], row[:, u:WORDS:HALVES], identity[:])
+            nc.scalar.copy(out=wo_pairs[:, k], in_=planes[:].rearrange("p x n -> p n x"))
 
         uv_grouped = grouped_pool.tile([P, K * PACK], BF16, tag="grouped", align_bytes=64)
         uv_by_code = uv_rows[:].rearrange("p t (m c) -> p c m t", c=PACK)
         for code in range(PACK):
             to = uv_grouped[:, code * K : (code + 1) * K].rearrange("p (m t) -> p m t", t=PACK)
-            if code in ():
-                nc.scalar.copy(out=to, in_=uv_by_code[:, code])
-            else:
-                nc.vector.tensor_copy(out=to, in_=uv_by_code[:, code])
+            nc.vector.tensor_copy(out=to, in_=uv_by_code[:, code])
         uv_codes = keep.tile([P, K], U32, align_bytes=64)
         uv_scales = keep.tile([P, K], U8, align_bytes=64)
         quantise(uv_grouped[:], uv_codes[:], uv_scales[:])
@@ -196,48 +126,35 @@ def tile_causalselfattention_pc_t_kernel(tc, y_lat, W_uv, W_o, out):
         v_scales = keep.tile([P, C], U8, align_bytes=64)
 
         def sort_y(n):
-            if NPRE == 0 or n < FIRST_SORTED:
+            if n < FIRST_SORTED:
                 return
-            first_word = (ROW_TILES - NPRE) * WORDS
+            h, j = units[n]["tiles"][-NPRE]
             y_sorted[n] = pre_pool.tile([P, NPRE, HALVES, P], F32, name="y_sorted")
-            per = NPRE // SORT_PIECES
-            for q in range(SORT_PIECES):
-                nc.gpsimd.tensor_copy(
-                    out=y_sorted[n][:, q * per : (q + 1) * per],
-                    in_=y_words[(n, "all")][:, first_word + q * per * WORDS : first_word + (q + 1) * per * WORDS].rearrange(
-                        "p (r w u) -> p r u w", r=per, u=HALVES
-                    ),
-                )
+            nc.gpsimd.tensor_copy(
+                out=y_sorted[n][:],
+                in_=y_words[units[n]["b"], h][:, j * WORDS : (j + NPRE) * WORDS].rearrange("p (r w u) -> p r u w", r=NPRE, u=HALVES),
+            )
 
         def transpose_y(n):
             y_grouped[n] = grouped_pool.tile([P, ROW_TILES * P * PACK], BF16, name="grouped", tag="grouped", align_bytes=64)
-            sources = []
-            for r, h in units[n]["rows"]:
-                if n in y_sorted and r >= ROW_TILES - NPRE:
-                    sources.append((y_sorted[n][:, r - (ROW_TILES - NPRE)], True))
-                else:
-                    sources.append((y_words[n][r], False))
+            sources = [(y_words[units[n]["b"], h][:, j * WORDS : (j + 1) * WORDS], False) for h, j in units[n]["tiles"]]
+            if n in y_sorted:
+                sources[-NPRE:] = [(y_sorted[n][:, r], True) for r in range(NPRE)]
             transpose_rows(sources, y_grouped[n][:])
 
         def quantise_y(n):
             y_codes[n] = mx_pool.tile([P, ROW_TILES * P], U32, name="y_codes", align_bytes=64)
             y_scales[n] = mx_pool.tile([P, ROW_TILES * P], U8, name="y_scales", align_bytes=64)
-            parts = units[n]["parts"]
-            width = ROW_TILES * P // parts
-            for q in range(parts):
-                columns = slice(q * width, (q + 1) * width)
-                quantise(
-                    y_grouped[n][:, q * width * PACK : (q + 1) * width * PACK], y_codes[n][:, columns], y_scales[n][:, columns]
-                )
+            quantise(y_grouped[n][:], y_codes[n][:], y_scales[n][:])
 
         def multiply_y(n):
             y_acc[n] = []
-            for bank in units[n]["banks"]:
-                acc = acc_pool.tile([P, len(bank["slots"]), HS], F32, tag="acc")
-                for g, s in enumerate(bank["slots"]):
-                    h = units[n]["rows"][s][1]
-                    tokens = slice(s * P, (s + 1) * P)
-                    head = slice(h * HS, (h + 1) * HS)
+            for first in range(0, ROW_TILES, GROUPS):
+                h, j = units[n]["tiles"][first]
+                head = slice(h * HS, (h + 1) * HS)
+                acc = acc_pool.tile([P, GROUPS, HS], F32, tag="acc")
+                for g in range(GROUPS):
+                    tokens = slice((first + g) * P, (first + g + 1) * P)
                     nc.tensor.matmul_mx(
                         out=acc[:, g, :],
                         lhsT=y_codes[n][:, tokens].bitcast(FP8X4),
@@ -247,18 +164,18 @@ def tile_causalselfattention_pc_t_kernel(tc, y_lat, W_uv, W_o, out):
                         start=True,
                         stop=True,
                     )
-                y_acc[n].append(acc)
+                y_acc[n].append((acc, results[units[n]["b"]][:, j : j + GROUPS, head]))
 
         def empty_y(n):
-            for j, bank in enumerate(units[n]["banks"]):
-                rows_of_out = bank["to"].shape[1]
-                source = y_acc[n][j][:].rearrange("p (i e) s -> p i (e s)", i=rows_of_out)
-                if False:
-                    nc.scalar.copy(out=bank["to"], in_=source)
-                else:
-                    nc.vector.tensor_copy(out=bank["to"], in_=source)
-                if bank["store"] is not None:
-                    store_rows(bank["store"])
+            for acc, to in y_acc[n]:
+                nc.vector.tensor_copy(out=to, in_=acc[:])
+
+        def store_y(n):
+            js = units[n]["store"]
+            if js is not None:
+                b, rows = units[n]["b"], slice(js[0], js[-1] + 1)
+                out_rows = out[b].rearrange("(p j) c -> p j c", j=ROW_TILES)
+                nc.sync.dma_start(out=out_rows[:, rows, :], in_=results[b][:, rows, :])
 
         transpose_y(0)
         sort_y(1)
@@ -279,18 +196,10 @@ def tile_causalselfattention_pc_t_kernel(tc, y_lat, W_uv, W_o, out):
                     stop=True,
                 )
             to = v_grouped[:, h * HS * PACK : (h + 1) * HS * PACK].rearrange("p (s t) -> p s t", t=PACK)
-            if h in ():
-                nc.scalar.copy(out=to, in_=v_acc[:].rearrange("p t s -> p s t"))
-            else:
-                nc.vector.tensor_copy(out=to, in_=v_acc[:].rearrange("p t s -> p s t"))
+            nc.vector.tensor_copy(out=to, in_=v_acc[:].rearrange("p t s -> p s t"))
         quantise(v_grouped[:], v_codes[:], v_scales[:])
 
         for step in range(1, UNITS + LAG):
-            while len(loaded) < len(load_groups) and False:
-                load_next()
-                if len(loaded) == len(load_groups):
-                    for held in held_stores:
-                        nc.sync.dma_start(out=held[0], in_=held[1])
             if step + 1 < UNITS:
                 sort_y(step + 1)
             if step < UNITS:
@@ -301,3 +210,4 @@ def tile_causalselfattention_pc_t_kernel(tc, y_lat, W_uv, W_o, out):
                 quantise_y(step - 1)
             if step >= LAG:
                 empty_y(step - LAG)
+                store_y(step - LAG)

@@ -23,7 +23,6 @@ PAIR = 2
 GROUPS = 4
 
 LAG = 2
-NPRE = 3
 FIRST_SORTED = 3
 
 FLOPS = 2 * K * K * C + 2 * B * NH * T * K * HS
@@ -75,7 +74,7 @@ def tile_causalselfattention_pc_t_kernel(tc, y_lat, W_uv, W_o, out):
                 units += [dict(b=b, tiles=[(h, j) for j in range(ROW_TILES)], store=None) for h in range(NH)]
                 units[-1]["store"] = range(ROW_TILES)
             else:
-                for js in (range(0, GROUPS), range(GROUPS, ROW_TILES)):
+                for js in (range(0, 4), range(4, 6), range(6, 8)):
                     units += [dict(b=b, tiles=[(h + e, j) for e in range(2) for j in js], store=None) for h in (0, 2)]
                     units[-1]["store"] = js
 
@@ -128,33 +127,41 @@ def tile_causalselfattention_pc_t_kernel(tc, y_lat, W_uv, W_o, out):
         def sort_y(n):
             if n < FIRST_SORTED:
                 return
-            h, j = units[n]["tiles"][-NPRE]
-            y_sorted[n] = pre_pool.tile([P, NPRE, HALVES, P], F32, name="y_sorted")
+            half = len(units[n]["tiles"]) // 2
+            h, j = units[n]["tiles"][half]
+            y_sorted[n] = pre_pool.tile([P, half, HALVES, P], F32, name="y_sorted")
             nc.gpsimd.tensor_copy(
                 out=y_sorted[n][:],
-                in_=y_words[units[n]["b"], h][:, j * WORDS : (j + NPRE) * WORDS].rearrange("p (r w u) -> p r u w", r=NPRE, u=HALVES),
+                in_=y_words[units[n]["b"], h][:, j * WORDS : (j + half) * WORDS].rearrange("p (r w u) -> p r u w", r=half, u=HALVES),
             )
 
         def transpose_y(n):
-            y_grouped[n] = grouped_pool.tile([P, ROW_TILES * P * PACK], BF16, name="grouped", tag="grouped", align_bytes=64)
+            y_grouped[n] = grouped_pool.tile([P, len(units[n]["tiles"]) * P * PACK], BF16, name="grouped", tag="grouped", align_bytes=64)
             sources = [(y_words[units[n]["b"], h][:, j * WORDS : (j + 1) * WORDS], False) for h, j in units[n]["tiles"]]
             if n in y_sorted:
-                sources[-NPRE:] = [(y_sorted[n][:, r], True) for r in range(NPRE)]
+                half = len(sources) // 2
+                sources[half:] = [(y_sorted[n][:, r], True) for r in range(half)]
             transpose_rows(sources, y_grouped[n][:])
 
         def quantise_y(n):
-            y_codes[n] = mx_pool.tile([P, ROW_TILES * P], U32, name="y_codes", align_bytes=64)
-            y_scales[n] = mx_pool.tile([P, ROW_TILES * P], U8, name="y_scales", align_bytes=64)
+            width = len(units[n]["tiles"]) * P
+            y_codes[n] = mx_pool.tile([P, width], U32, name="y_codes", align_bytes=64)
+            y_scales[n] = mx_pool.tile([P, width], U8, name="y_scales", align_bytes=64)
             quantise(y_grouped[n][:], y_codes[n][:], y_scales[n][:])
 
         def multiply_y(n):
             y_acc[n] = []
-            for first in range(0, ROW_TILES, GROUPS):
-                h, j = units[n]["tiles"][first]
-                head = slice(h * HS, (h + 1) * HS)
+            tiles = units[n]["tiles"]
+            slots = list(range(len(tiles)))
+            if len(tiles) == GROUPS:
+                slots = [0, 2, 1, 3]
+            for first in range(0, len(tiles), GROUPS):
+                bank = slots[first : first + GROUPS]
                 acc = acc_pool.tile([P, GROUPS, HS], F32, tag="acc")
-                for g in range(GROUPS):
-                    tokens = slice((first + g) * P, (first + g + 1) * P)
+                for g, slot in enumerate(bank):
+                    h, j = tiles[slot]
+                    tokens = slice(slot * P, (slot + 1) * P)
+                    head = slice(h * HS, (h + 1) * HS)
                     nc.tensor.matmul_mx(
                         out=acc[:, g, :],
                         lhsT=y_codes[n][:, tokens].bitcast(FP8X4),
@@ -164,11 +171,13 @@ def tile_causalselfattention_pc_t_kernel(tc, y_lat, W_uv, W_o, out):
                         start=True,
                         stop=True,
                     )
-                y_acc[n].append((acc, results[units[n]["b"]][:, j : j + GROUPS, head]))
+                (h, j), (last_h, last_j) = tiles[bank[0]], tiles[bank[-1]]
+                to = results[units[n]["b"]][:, j : last_j + 1, h * HS : (last_h + 1) * HS]
+                y_acc[n].append((acc[:].rearrange("p (j e) s -> p j (e s)", j=last_j + 1 - j), to))
 
         def empty_y(n):
             for acc, to in y_acc[n]:
-                nc.vector.tensor_copy(out=to, in_=acc[:])
+                nc.vector.tensor_copy(out=to, in_=acc)
 
         def store_y(n):
             js = units[n]["store"]
@@ -199,14 +208,14 @@ def tile_causalselfattention_pc_t_kernel(tc, y_lat, W_uv, W_o, out):
             nc.vector.tensor_copy(out=to, in_=v_acc[:].rearrange("p t s -> p s t"))
         quantise(v_grouped[:], v_codes[:], v_scales[:])
 
-        for step in range(1, UNITS + LAG):
-            if step + 1 < UNITS:
+        for step in range(1, len(units) + LAG):
+            if step + 1 < len(units):
                 sort_y(step + 1)
-            if step < UNITS:
+            if step < len(units):
                 transpose_y(step)
             if step >= LAG:
                 multiply_y(step - LAG)
-            if step - 1 < UNITS:
+            if step - 1 < len(units):
                 quantise_y(step - 1)
             if step >= LAG:
                 empty_y(step - LAG)

@@ -23,6 +23,7 @@ PAIR = 2
 GROUPS = 4
 
 LAG = 2
+SORTED = {8: 3, 4: 2}
 FIRST_SORTED = 3
 
 FLOPS = 2 * K * K * C + 2 * B * NH * T * K * HS
@@ -81,7 +82,6 @@ def tile_causalselfattention_pc_t_kernel(tc, y_lat, W_uv, W_o, out):
         wo_rows = y_pool.tile([P, NH * K], BF16, name="y_rows")
         uv_rows = y_pool.tile([P, PACK, K], BF16, name="y_rows")
         nc.sync.dma_start(out=wo_rows[:], in_=W_o.rearrange("(n i) j -> n (i j)", i=NH))
-        nc.sync.dma_start(out=uv_rows[:], in_=W_uv.rearrange("(p t) l -> p t l", t=PACK))
 
         y_words = {}
         for first in list(range(2 * NH)) + list(range(2 * NH, UNITS, 2)):
@@ -96,6 +96,8 @@ def tile_causalselfattention_pc_t_kernel(tc, y_lat, W_uv, W_o, out):
             words = rows[:].bitcast(F32)
             for k in range(heads):
                 y_words[b, h + k] = words[:, k * ROW_TILES * WORDS : (k + 1) * ROW_TILES * WORDS]
+            if first == 0:
+                nc.sync.dma_start(out=uv_rows[:], in_=W_uv.rearrange("(p t) l -> p t l", t=PACK))
 
         wo_words = wo_rows[:].bitcast(F32)
         wo_grouped = grouped_pool.tile([P, NH * P * PACK], BF16, tag="grouped", align_bytes=64)
@@ -108,17 +110,21 @@ def tile_causalselfattention_pc_t_kernel(tc, y_lat, W_uv, W_o, out):
                     nc.tensor.transpose(planes[:, HALVES * e + u, :], row[:, u:WORDS:HALVES], identity[:])
             nc.scalar.copy(out=wo_pairs[:, k], in_=planes[:].rearrange("p x n -> p n x"))
 
-        uv_grouped = grouped_pool.tile([P, K * PACK], BF16, tag="grouped", align_bytes=64)
-        uv_by_code = uv_rows[:].rearrange("p t (m c) -> p c m t", c=PACK)
-        for code in range(PACK):
-            to = uv_grouped[:, code * K : (code + 1) * K].rearrange("p (m t) -> p m t", t=PACK)
-            nc.vector.tensor_copy(out=to, in_=uv_by_code[:, code])
-        uv_codes = keep.tile([P, K], U32, align_bytes=64)
-        uv_scales = keep.tile([P, K], U8, align_bytes=64)
-        quantise(uv_grouped[:], uv_codes[:], uv_scales[:])
         wo_codes = keep.tile([P, C], U32, align_bytes=64)
         wo_scales = keep.tile([P, C], U8, align_bytes=64)
         quantise(wo_grouped[:], wo_codes[:], wo_scales[:])
+
+        uv_grouped = grouped_pool.tile([P, K * PACK], BF16, tag="grouped", align_bytes=64)
+        uv_by_code = uv_rows[:].rearrange("p t (m c) -> p c m t", c=PACK)
+        uv_codes = keep.tile([P, K], U32, align_bytes=64)
+        uv_scales = keep.tile([P, K], U8, align_bytes=64)
+        for chunk in range(PACK + 1):
+            if chunk < PACK:
+                to = uv_grouped[:, chunk * K : (chunk + 1) * K].rearrange("p (m t) -> p m t", t=PACK)
+                nc.vector.tensor_copy(out=to, in_=uv_by_code[:, chunk])
+            if chunk > 0:
+                columns = slice((chunk - 1) * P, chunk * P)
+                quantise(uv_grouped[:, (chunk - 1) * K : chunk * K], uv_codes[:, columns], uv_scales[:, columns])
 
         y_sorted, y_grouped, y_codes, y_scales, y_acc = {}, {}, {}, {}, {}
         v_codes = keep.tile([P, C], U32, align_bytes=64)
@@ -127,20 +133,20 @@ def tile_causalselfattention_pc_t_kernel(tc, y_lat, W_uv, W_o, out):
         def sort_y(n):
             if n < FIRST_SORTED:
                 return
-            half = len(units[n]["tiles"]) // 2
-            h, j = units[n]["tiles"][half]
-            y_sorted[n] = pre_pool.tile([P, half, HALVES, P], F32, name="y_sorted")
+            count = SORTED[len(units[n]["tiles"])]
+            h, j = units[n]["tiles"][-count]
+            y_sorted[n] = pre_pool.tile([P, count, HALVES, P], F32, name="y_sorted")
             nc.gpsimd.tensor_copy(
                 out=y_sorted[n][:],
-                in_=y_words[units[n]["b"], h][:, j * WORDS : (j + half) * WORDS].rearrange("p (r w u) -> p r u w", r=half, u=HALVES),
+                in_=y_words[units[n]["b"], h][:, j * WORDS : (j + count) * WORDS].rearrange("p (r w u) -> p r u w", r=count, u=HALVES),
             )
 
         def transpose_y(n):
             y_grouped[n] = grouped_pool.tile([P, len(units[n]["tiles"]) * P * PACK], BF16, name="grouped", tag="grouped", align_bytes=64)
             sources = [(y_words[units[n]["b"], h][:, j * WORDS : (j + 1) * WORDS], False) for h, j in units[n]["tiles"]]
             if n in y_sorted:
-                half = len(sources) // 2
-                sources[half:] = [(y_sorted[n][:, r], True) for r in range(half)]
+                count = SORTED[len(sources)]
+                sources[-count:] = [(y_sorted[n][:, r], True) for r in range(count)]
             transpose_rows(sources, y_grouped[n][:])
 
         def quantise_y(n):
@@ -177,7 +183,10 @@ def tile_causalselfattention_pc_t_kernel(tc, y_lat, W_uv, W_o, out):
 
         def empty_y(n):
             for acc, to in y_acc[n]:
-                nc.vector.tensor_copy(out=to, in_=acc)
+                if n in (len(units) - 3, len(units) - 1):
+                    nc.scalar.copy(out=to, in_=acc)
+                else:
+                    nc.vector.tensor_copy(out=to, in_=acc)
 
         def store_y(n):
             js = units[n]["store"]
@@ -190,13 +199,16 @@ def tile_causalselfattention_pc_t_kernel(tc, y_lat, W_uv, W_o, out):
         sort_y(1)
 
         v_grouped = grouped_pool.tile([P, C * PACK], BF16, tag="grouped", align_bytes=64)
+        v_acc = []
         for h in range(NH):
-            head = slice(h * HS, (h + 1) * HS)
-            v_acc = acc_pool.tile([P, PACK, HS], F32, tag="acc")
-            for code in range(PACK):
-                latent = slice(code * P, (code + 1) * P)
+            acc = acc_pool.tile([P, PACK, HS], F32, name="v_acc", tag="acc")
+            v_acc.append(acc)
+        for code in range(PACK):
+            latent = slice(code * P, (code + 1) * P)
+            for h in range(NH):
+                head = slice(h * HS, (h + 1) * HS)
                 nc.tensor.matmul_mx(
-                    out=v_acc[:, code, :],
+                    out=v_acc[h][:, code, :],
                     lhsT=uv_codes[:, latent].bitcast(FP8X4),
                     lhsT_scale=uv_scales[:, latent],
                     rhs=wo_codes[:, head].bitcast(FP8X4),
@@ -204,8 +216,13 @@ def tile_causalselfattention_pc_t_kernel(tc, y_lat, W_uv, W_o, out):
                     start=True,
                     stop=True,
                 )
+        for h in range(NH):
             to = v_grouped[:, h * HS * PACK : (h + 1) * HS * PACK].rearrange("p (s t) -> p s t", t=PACK)
-            nc.vector.tensor_copy(out=to, in_=v_acc[:].rearrange("p t s -> p s t"))
+            by_word = v_acc[h][:].rearrange("p t s -> p s t")
+            if h % 2 == 0:
+                nc.vector.tensor_copy(out=to, in_=by_word)
+            else:
+                nc.scalar.copy(out=to, in_=by_word)
         quantise(v_grouped[:], v_codes[:], v_scales[:])
 
         for step in range(1, len(units) + LAG):

@@ -24,6 +24,7 @@ GROUPS = 4
 
 LAG = 2
 SORTED = {8: 3, 4: 2}
+FIRST_PAIRED = 6
 FIRST_SORTED = 3
 
 FLOPS = 2 * K * K * C + 2 * B * NH * T * K * HS
@@ -71,31 +72,33 @@ def tile_causalselfattention_pc_t_kernel(tc, y_lat, W_uv, W_o, out):
         for b in range(B):
             result = res_pool.tile([P, ROW_TILES, C], F32, name="result_%d" % b)
             results.append(result)
-            if b < B - 1:
-                units += [dict(b=b, tiles=[(h, j) for j in range(ROW_TILES)], store=None) for h in range(NH)]
-                units[-1]["store"] = range(ROW_TILES)
-            else:
-                for js in (range(0, 4), range(4, 6), range(6, 8)):
-                    units += [dict(b=b, tiles=[(h + e, j) for e in range(2) for j in js], store=None) for h in (0, 2)]
+            cuts = (range(0, 4), range(4, 8)) if b < B - 1 else (range(0, 4), range(4, 6), range(6, 8))
+            singles = [h for h in range(NH) if b * NH + h < FIRST_PAIRED]
+            pairs = [h for h in range(len(singles), NH, 2)]
+            order = [(h, js) for h in pairs for js in cuts] if b < B - 1 else [(h, js) for js in cuts for h in pairs]
+            units += [dict(b=b, first=h, tiles=[(h, j) for j in range(ROW_TILES)], js=None, store=None) for h in singles]
+            for h, js in order:
+                units.append(dict(b=b, first=h, tiles=[(h + a, j) for a in range(2) for j in js], js=js, store=None))
+                if b == B - 1 and h == pairs[-1]:
                     units[-1]["store"] = js
+            if b < B - 1:
+                units[-1]["store"] = range(ROW_TILES)
 
         wo_rows = y_pool.tile([P, NH * K], BF16, name="y_rows")
         uv_rows = y_pool.tile([P, PACK, K], BF16, name="y_rows")
         nc.sync.dma_start(out=wo_rows[:], in_=W_o.rearrange("(n i) j -> n (i j)", i=NH))
 
+        flat_y = y_lat.rearrange("b h t l -> (b h t) l")
         y_words = {}
-        for first in list(range(2 * NH)) + list(range(2 * NH, UNITS, 2)):
-            b, h = first // NH, first % NH
-            heads = 1 if b < 2 else 2
+        for first in list(range(FIRST_PAIRED)) + list(range(FIRST_PAIRED, UNITS, 2)):
+            heads = 1 if first < FIRST_PAIRED else 2
             pool = y_pool if heads == 1 else pair_pool
             rows = pool.tile([P, heads * ROW_TILES * K], BF16, name="y_rows")
             nc.sync.dma_start(
-                out=rows[:].rearrange("p (h x) -> p h x", h=heads),
-                in_=y_lat[b, h : h + heads].rearrange("h (p j) l -> p h (j l)", j=ROW_TILES),
+                out=rows[:],
+                in_=flat_y[first * T : (first + heads) * T, :].rearrange("(p r) l -> p (r l)", r=heads * ROW_TILES),
             )
-            words = rows[:].bitcast(F32)
-            for k in range(heads):
-                y_words[b, h + k] = words[:, k * ROW_TILES * WORDS : (k + 1) * ROW_TILES * WORDS]
+            y_words[first // NH, first % NH] = rows[:].bitcast(F32)
             if first == 0:
                 nc.sync.dma_start(out=uv_rows[:], in_=W_uv.rearrange("(p t) l -> p t l", t=PACK))
 
@@ -133,21 +136,41 @@ def tile_causalselfattention_pc_t_kernel(tc, y_lat, W_uv, W_o, out):
         def sort_y(n):
             if n < FIRST_SORTED:
                 return
-            count = SORTED[len(units[n]["tiles"])]
-            h, j = units[n]["tiles"][-count]
+            unit = units[n]
+            count = SORTED[len(unit["tiles"])]
+            r = ROW_TILES - count if unit["js"] is None else ROW_TILES + unit["js"][-count]
             y_sorted[n] = pre_pool.tile([P, count, HALVES, P], F32, name="y_sorted")
             nc.gpsimd.tensor_copy(
                 out=y_sorted[n][:],
-                in_=y_words[units[n]["b"], h][:, j * WORDS : (j + count) * WORDS].rearrange("p (r w u) -> p r u w", r=count, u=HALVES),
+                in_=y_words[unit["b"], unit["first"]][:, r * WORDS : (r + count) * WORDS].rearrange(
+                    "p (r w u) -> p r u w", r=count, u=HALVES
+                ),
             )
 
         def transpose_y(n):
-            y_grouped[n] = grouped_pool.tile([P, len(units[n]["tiles"]) * P * PACK], BF16, name="grouped", tag="grouped", align_bytes=64)
-            sources = [(y_words[units[n]["b"], h][:, j * WORDS : (j + 1) * WORDS], False) for h, j in units[n]["tiles"]]
-            if n in y_sorted:
-                count = SORTED[len(sources)]
-                sources[-count:] = [(y_sorted[n][:, r], True) for r in range(count)]
-            transpose_rows(sources, y_grouped[n][:])
+            unit = units[n]
+            tiles = len(unit["tiles"])
+            words = y_words[unit["b"], unit["first"]]
+            y_grouped[n] = grouped_pool.tile([P, tiles * P * PACK], BF16, name="grouped", tag="grouped", align_bytes=64)
+            count = SORTED[tiles] if n in y_sorted else 0
+            if unit["js"] is None:
+                sources = [(words[:, r * WORDS : (r + 1) * WORDS], False) for r in range(ROW_TILES - count)]
+                sources += [(y_sorted[n][:, q], True) for q in range(count)]
+                transpose_rows(sources, y_grouped[n][:])
+                return
+            by_group = y_grouped[n][:].bitcast(F32).rearrange("p (a g n x) -> p g a n x", a=2, g=tiles // 2, x=2 * HALVES)
+            for g, j in enumerate(unit["js"]):
+                planes = planes_pool.tile([P, 2 * HALVES, P], F32, tag="planes")
+                for i in range(2):
+                    r = ROW_TILES * i + j
+                    q = g - (tiles // 2 - count)
+                    for u in range(HALVES):
+                        if i == 1 and q >= 0:
+                            source = y_sorted[n][:, q, u, :]
+                        else:
+                            source = words[:, r * WORDS + u : (r + 1) * WORDS : HALVES]
+                        nc.tensor.transpose(planes[:, HALVES * i + u, :], source, identity[:])
+                nc.scalar.copy(out=by_group[:, g], in_=planes[:].rearrange("p x (a n) -> p a n x", a=2))
 
         def quantise_y(n):
             width = len(units[n]["tiles"]) * P

@@ -25,6 +25,7 @@ GROUPS = 4
 LAG = 2
 SORTED = {8: 3, 4: 2}
 FIRST_PAIRED = 6
+FIRST_CUT = 2
 FIRST_SORTED = 3
 
 FLOPS = 2 * K * K * C + 2 * B * NH * T * K * HS
@@ -79,9 +80,9 @@ def tile_causalselfattention_pc_t_kernel(tc, y_lat, W_uv, W_o, out):
             units += [dict(b=b, first=h, tiles=[(h, j) for j in range(ROW_TILES)], js=None, store=None) for h in singles]
             for h, js in order:
                 units.append(dict(b=b, first=h, tiles=[(h + a, j) for a in range(2) for j in js], js=js, store=None))
-                if b == B - 1 and h == pairs[-1]:
+                if b >= FIRST_CUT and h == pairs[-1]:
                     units[-1]["store"] = js
-            if b < B - 1:
+            if b < FIRST_CUT:
                 units[-1]["store"] = range(ROW_TILES)
 
         wo_rows = y_pool.tile([P, NH * K], BF16, name="y_rows")

from contextlib import ExitStack

import concourse.mybir as mybir
from concourse.masks import make_identity

BF16 = mybir.dt.bfloat16
F32 = mybir.dt.float32
U32 = mybir.dt.uint32
U8 = mybir.dt.uint8
FP8X4 = mybir.dt.float8_e4m3fn_x4

P = 128
PACK = 4
K = P * PACK
WORDS = K // 2
HALVES = WORDS // P

B, NH, T, HS = 4, 4, 1024, 128
C = NH * HS
UNITS = B * NH
ROW_TILES = 8
PAIR = 2
GROUPS = 4

LAG = 2
SORTED = {8: 3, 4: 2}
FIRST_PAIRED = 6
FIRST_CUT = 2
FIRST_SORTED = 3

FLOPS = 2 * K * K * C + 2 * B * NH * T * K * HS


def tile_causalselfattention_pc_t_kernel(tc, y_lat, W_uv, W_o, out):
    nc = tc.nc
    with ExitStack() as ctx:
        keep = ctx.enter_context(tc.tile_pool(name="keep", bufs=1))
        y_pool = ctx.enter_context(tc.tile_pool(name="y_rows", bufs=5))
        pair_pool = ctx.enter_context(tc.tile_pool(name="y_pairs", bufs=4))
        res_pool = ctx.enter_context(tc.tile_pool(name="result", bufs=1))
        mx_pool = ctx.enter_context(tc.tile_pool(name="mx", bufs=3))
        grouped_pool = ctx.enter_context(tc.tile_pool(name="grouped", bufs=3))
        pre_pool = ctx.enter_context(tc.tile_pool(name="sorted", bufs=2))
        planes_pool = ctx.enter_context(tc.psum_pool(name="planes", bufs=4))
        acc_pool = ctx.enter_context(tc.psum_pool(name="acc", bufs=4))
        ctx.enter_context(tc.manual_schedule())

        identity = keep.tile([P, P], F32)
        make_identity(nc, identity[:])

        def transpose_rows(sources, grouped):
            grouped_words = grouped.bitcast(F32)
            bank_words = PAIR * P * HALVES
            for pair in range(len(sources) // PAIR):
                planes = planes_pool.tile([P, HALVES, PAIR * P], F32, tag="planes")
                for i in range(PAIR):
                    words, is_sorted = sources[pair * PAIR + i]
                    for u in range(HALVES):
                        source = words[:, u, :] if is_sorted else words[:, u:WORDS:HALVES]
                        nc.tensor.transpose(planes[:, u, i * P : (i + 1) * P], source, identity[:])
                nc.scalar.copy(
                    out=grouped_words[:, pair * bank_words : (pair + 1) * bank_words].rearrange(
                        "p (n u) -> p n u", u=HALVES
                    ),
                    in_=planes[:].rearrange("p u n -> p n u"),
                )

        def quantise(grouped, codes, scales):
            nc.vector.quantize_mx(out=codes.bitcast(FP8X4), scales=scales, in_=grouped)

        units = []
        results = []
        for b in range(B):
            result = res_pool.tile([P, ROW_TILES, C], F32, name="result_%d" % b)
            results.append(result)
            cuts = (range(0, 4), range(4, 8)) if b < B - 1 else (range(0, 4), range(4, 6), range(6, 8))
            singles = [h for h in range(NH) if b * NH + h < FIRST_PAIRED]
            pairs = [h for h in range(len(singles), NH, 2)]
            order = [(h, js) for h in pairs for js in cuts] if b < B - 1 else [(h, js) for js in cuts for h in pairs]
            units += [dict(b=b, first=h, tiles=[(h, j) for j in range(ROW_TILES)], js=None, store=None) for h in singles]
            for h, js in order:
                units.append(dict(b=b, first=h, tiles=[(h + a, j) for a in range(2) for j in js], js=js, store=None))
                if b >= FIRST_CUT and h == pairs[-1]:
                    units[-1]["store"] = js
            if b < FIRST_CUT:
                units[-1]["store"] = range(ROW_TILES)

        wo_rows = y_pool.tile([P, NH * K], BF16, name="y_rows")
        uv_rows = y_pool.tile([P, PACK, K], BF16, name="y_rows")
        nc.sync.dma_start(out=wo_rows[:], in_=W_o.rearrange("(n i) j -> n (i j)", i=NH))

        flat_y = y_lat.rearrange("b h t l -> (b h t) l")
        y_words = {}
        for first in list(range(FIRST_PAIRED)) + list(range(FIRST_PAIRED, UNITS, 2)):
            heads = 1 if first < FIRST_PAIRED else 2
            pool = y_pool if heads == 1 else pair_pool
            rows = pool.tile([P, heads * ROW_TILES * K], BF16, name="y_rows")
            nc.sync.dma_start(
                out=rows[:],
                in_=flat_y[first * T : (first + heads) * T, :].rearrange("(p r) l -> p (r l)", r=heads * ROW_TILES),
            )
            y_words[first // NH, first % NH] = rows[:].bitcast(F32)
            if first == 0:
                nc.sync.dma_start(out=uv_rows[:], in_=W_uv.rearrange("(p t) l -> p t l", t=PACK))

        wo_words = wo_rows[:].bitcast(F32)
        wo_grouped = grouped_pool.tile([P, NH * P * PACK], BF16, tag="grouped", align_bytes=64)
        wo_pairs = wo_grouped[:].bitcast(F32).rearrange("p (n k x) -> p k n x", k=NH // PAIR, x=PAIR * HALVES)
        for k in range(NH // PAIR):
            planes = planes_pool.tile([P, PAIR * HALVES, P], F32, tag="planes")
            for e in range(PAIR):
                row = wo_words[:, (PAIR * k + e) * WORDS : (PAIR * k + e + 1) * WORDS]
                for u in range(HALVES):
                    nc.tensor.transpose(planes[:, HALVES * e + u, :], row[:, u:WORDS:HALVES], identity[:])
            nc.scalar.copy(out=wo_pairs[:, k], in_=planes[:].rearrange("p x n -> p n x"))

        wo_codes = keep.tile([P, C], U32, align_bytes=64)
        wo_scales = keep.tile([P, C], U8, align_bytes=64)
        quantise(wo_grouped[:], wo_codes[:], wo_scales[:])

        uv_grouped = grouped_pool.tile([P, K * PACK], BF16, tag="grouped", align_bytes=64)
        uv_by_code = uv_rows[:].rearrange("p t (m c) -> p c m t", c=PACK)
        uv_codes = keep.tile([P, K], U32, align_bytes=64)
        uv_scales = keep.tile([P, K], U8, align_bytes=64)
        for chunk in range(PACK + 1):
            if chunk < PACK:
                to = uv_grouped[:, chunk * K : (chunk + 1) * K].rearrange("p (m t) -> p m t", t=PACK)
                nc.vector.tensor_copy(out=to, in_=uv_by_code[:, chunk])
            if chunk > 0:
                columns = slice((chunk - 1) * P, chunk * P)
                quantise(uv_grouped[:, (chunk - 1) * K : chunk * K], uv_codes[:, columns], uv_scales[:, columns])

        y_sorted, y_grouped, y_codes, y_scales, y_acc = {}, {}, {}, {}, {}
        v_codes = keep.tile([P, C], U32, align_bytes=64)
        v_scales = keep.tile([P, C], U8, align_bytes=64)

        def sort_y(n):
            if n < FIRST_SORTED:
                return
            unit = units[n]
            count = SORTED[len(unit["tiles"])]
            r = ROW_TILES - count if unit["js"] is None else ROW_TILES + unit["js"][-count]
            y_sorted[n] = pre_pool.tile([P, count, HALVES, P], F32, name="y_sorted")
            nc.gpsimd.tensor_copy(
                out=y_sorted[n][:],
                in_=y_words[unit["b"], unit["first"]][:, r * WORDS : (r + count) * WORDS].rearrange(
                    "p (r w u) -> p r u w", r=count, u=HALVES
                ),
            )

        def transpose_y(n):
            unit = units[n]
            tiles = len(unit["tiles"])
            words = y_words[unit["b"], unit["first"]]
            y_grouped[n] = grouped_pool.tile([P, tiles * P * PACK], BF16, name="grouped", tag="grouped", align_bytes=64)
            count = SORTED[tiles] if n in y_sorted else 0
            if unit["js"] is None:
                sources = [(words[:, r * WORDS : (r + 1) * WORDS], False) for r in range(ROW_TILES - count)]
                sources += [(y_sorted[n][:, q], True) for q in range(count)]
                transpose_rows(sources, y_grouped[n][:])
                return
            by_group = y_grouped[n][:].bitcast(F32).rearrange("p (a g n x) -> p g a n x", a=2, g=tiles // 2, x=2 * HALVES)
            for g, j in enumerate(unit["js"]):
                planes = planes_pool.tile([P, 2 * HALVES, P], F32, tag="planes")
                for i in range(2):
                    r = ROW_TILES * i + j
                    q = g - (tiles // 2 - count)
                    for u in range(HALVES):
                        if i == 1 and q >= 0:
                            source = y_sorted[n][:, q, u, :]
                        else:
                            source = words[:, r * WORDS + u : (r + 1) * WORDS : HALVES]
                        nc.tensor.transpose(planes[:, HALVES * i + u, :], source, identity[:])
                nc.scalar.copy(out=by_group[:, g], in_=planes[:].rearrange("p x (a n) -> p a n x", a=2))

        def quantise_y(n):
            width = len(units[n]["tiles"]) * P
            y_codes[n] = mx_pool.tile([P, width], U32, name="y_codes", align_bytes=64)
            y_scales[n] = mx_pool.tile([P, width], U8, name="y_scales", align_bytes=64)
            quantise(y_grouped[n][:], y_codes[n][:], y_scales[n][:])

        def multiply_y(n):
            y_acc[n] = []
            tiles = units[n]["tiles"]
            slots = list(range(len(tiles)))
            if len(tiles) == GROUPS:
                slots = [0, 2, 1, 3]
            for first in range(0, len(tiles), GROUPS):
                bank = slots[first : first + GROUPS]
                acc = acc_pool.tile([P, GROUPS, HS], F32, tag="acc")
                for g, slot in enumerate(bank):
                    h, j = tiles[slot]
                    tokens = slice(slot * P, (slot + 1) * P)
                    head = slice(h * HS, (h + 1) * HS)
                    nc.tensor.matmul_mx(
                        out=acc[:, g, :],
                        lhsT=y_codes[n][:, tokens].bitcast(FP8X4),
                        lhsT_scale=y_scales[n][:, tokens],
                        rhs=v_codes[:, head].bitcast(FP8X4),
                        rhs_scale=v_scales[:, head],
                        start=True,
                        stop=True,
                    )
                (h, j), (last_h, last_j) = tiles[bank[0]], tiles[bank[-1]]
                to = results[units[n]["b"]][:, j : last_j + 1, h * HS : (last_h + 1) * HS]
                y_acc[n].append((acc[:].rearrange("p (j e) s -> p j (e s)", j=last_j + 1 - j), to))

        def empty_y(n):
            for acc, to in y_acc[n]:
                if n in (len(units) - 3, len(units) - 1):
                    nc.scalar.copy(out=to, in_=acc)
                else:
                    nc.vector.tensor_copy(out=to, in_=acc)

        def store_y(n):
            js = units[n]["store"]
            if js is not None:
                b, rows = units[n]["b"], slice(js[0], js[-1] + 1)
                out_rows = out[b].rearrange("(p j) c -> p j c", j=ROW_TILES)
                nc.sync.dma_start(out=out_rows[:, rows, :], in_=results[b][:, rows, :])

        transpose_y(0)
        sort_y(1)

        v_grouped = grouped_pool.tile([P, C * PACK], BF16, tag="grouped", align_bytes=64)
        v_acc = []
        for h in range(NH):
            acc = acc_pool.tile([P, PACK, HS], F32, name="v_acc", tag="acc")
            v_acc.append(acc)
        for code in range(PACK):
            latent = slice(code * P, (code + 1) * P)
            for h in range(NH):
                head = slice(h * HS, (h + 1) * HS)
                nc.tensor.matmul_mx(
                    out=v_acc[h][:, code, :],
                    lhsT=uv_codes[:, latent].bitcast(FP8X4),
                    lhsT_scale=uv_scales[:, latent],
                    rhs=wo_codes[:, head].bitcast(FP8X4),
                    rhs_scale=wo_scales[:, head],
                    start=True,
                    stop=True,
                )
        for h in range(NH):
            to = v_grouped[:, h * HS * PACK : (h + 1) * HS * PACK].rearrange("p (s t) -> p s t", t=PACK)
            by_word = v_acc[h][:].rearrange("p t s -> p s t")
            if h % 2 == 0:
                nc.vector.tensor_copy(out=to, in_=by_word)
            else:
                nc.scalar.copy(out=to, in_=by_word)
        quantise(v_grouped[:], v_codes[:], v_scales[:])

        for step in range(1, len(units) + LAG):
            if step + 1 < len(units):
                sort_y(step + 1)
            if step < len(units):
                transpose_y(step)
            if step >= LAG:
                multiply_y(step - LAG)
            if step - 1 < len(units):
                quantise_y(step - 1)
            if step >= LAG:
                empty_y(step - LAG)
                store_y(step - LAG)
